import numpy as np
import ml_dtypes


def mxq(x, axis, fmt="e4m3"):
    dtype, down = {"e4m3": (ml_dtypes.float8_e4m3fn, 7), "e5m2": (ml_dtypes.float8_e5m2, 14)}[fmt]
    v = np.moveaxis(np.asarray(x, np.float32).astype(ml_dtypes.bfloat16).astype(np.float64), axis, -1)
    blocks = v.reshape(v.shape[:-1] + (-1, 32))
    amax = np.abs(blocks).max(-1, keepdims=True)
    byte = np.maximum(np.where(amax > 0, np.frexp(amax)[1] - 1 + 127, 0) - down, 1)
    scale = np.exp2(byte - 127.0)
    codes = (blocks / scale).astype(np.float32).astype(dtype).astype(np.float64)
    return np.moveaxis((codes * scale).reshape(v.shape), -1, axis)


WIDE = False


def mx_kscale(k):
    if not WIDE:
        return np.ones(k)
    levels = np.array([10, -10, 5, -5, 0])
    a = np.random.permutation(np.resize(levels, k // 512 * 4)).reshape(k // 512, 4)
    idx = np.arange(k)
    return np.exp2(a[idx // 512, idx % 128 // 32])


BF16 = ml_dtypes.bfloat16


def bf(x):
    return np.asarray(x, np.float32).astype(BF16)


def f64(x):
    return np.asarray(x).astype(np.float64)


B, C, D, R, STEPS = 4096, 1024, 512, 4, 5
EPS = 1e-8


def shared_mix(n, u):
    return sum(np.random.standard_normal((n, 1)) * u[r] for r in range(R))


def setup_inputs():
    u = np.random.standard_normal((R, D)) / np.sqrt(R)
    s = mx_kscale(D)
    r = (s / s.max())[np.arange(B) * D // B][:, None]
    current = (0.6 * shared_mix(B, u) + 0.45 * np.random.standard_normal((B, D))) * r
    memory = 2.4 * shared_mix(C, u) + 1.8 * np.random.standard_normal((C, D))
    return {"current": bf(current), "memory_matrix": bf(memory)}


def reference(current, memory_matrix):
    cur, mem = f64(current), f64(memory_matrix)
    mem_norm = np.maximum(np.sqrt((mem * mem).sum(-1)), EPS)
    cur_norm = np.maximum(np.sqrt((cur * cur).sum(-1, keepdims=True)), EPS)
    sim = (mxq(cur, 1, "e4m3") @ mxq(mem, 1, "e4m3").T) / (cur_norm * mem_norm[None, :])
    e = np.exp(sim - sim.max(-1, keepdims=True))
    attracted = (mxq(e, 1, "e4m3") @ mxq(mem, 0, "e4m3")) / e.sum(-1, keepdims=True)
    return 0.8 * attracted + 0.2 * cur

@@ -1,0 +1,258 @@
+from contextlib import ExitStack
+
+import concourse.mybir as mybir
+from concourse.masks import make_identity
+
+F32 = mybir.dt.float32
+BF16 = mybir.dt.bfloat16
+U32 = mybir.dt.uint32
+U8 = mybir.dt.uint8
+FP8X4 = mybir.dt.float8_e4m3fn_x4
+ALU = mybir.AluOpType
+FN = mybir.ActivationFunctionType
+AXIS_X = mybir.AxisListType.X
+
+P = 128
+B, C, D = 4096, 1024, 512
+TILES = B // P
+CHUNK = 4
+CHUNKS = TILES // CHUNK
+EPS = 1e-8
+FLOPS = 2 * B * C * D * 2
+
+E1_ON_VECTOR = True
+CURCOPY_ON_VECTOR = (0, 1, 2)
+C1_ON_VECTOR = ()
+
+
+def tile_ca3_recurrentmatrix_pa_t_kernel(tc, current, memory_matrix, out):
+    nc = tc.nc
+    cur_rows = current.rearrange("(p t) d -> p (t d)", t=TILES)
+    out_rows = out.rearrange("(p t) d -> p (t d)", t=TILES)
+    mem_rows = memory_matrix.rearrange("(j p) d -> p j d", p=P)
+
+    with ExitStack() as stack:
+        keep = stack.enter_context(tc.tile_pool(name="keep", bufs=1))
+        junkp = stack.enter_context(tc.tile_pool(name="junkp", bufs=2))
+        gcp = stack.enter_context(tc.tile_pool(name="gcp", bufs=2))
+        yp = stack.enter_context(tc.tile_pool(name="yp", bufs=6))
+        ep = stack.enter_context(tc.tile_pool(name="ep", bufs=3))
+        small = stack.enter_context(tc.tile_pool(name="small", bufs=8))
+        c02p = stack.enter_context(tc.tile_pool(name="c02p", bufs=3))
+        op = stack.enter_context(tc.tile_pool(name="op", bufs=3))
+        ps_sim = stack.enter_context(tc.psum_pool(name="ps_sim", bufs=4))
+        ps_tr = stack.enter_context(tc.psum_pool(name="ps_tr", bufs=2))
+        ps_acc = stack.enter_context(tc.psum_pool(name="ps_acc", bufs=2))
+
+        mem_sb = keep.tile([P, 8 * D], BF16)
+        mem_v = mem_sb[:].rearrange("p (j d) -> p j d", j=8)
+        for h in range(2):
+            nc.sync.dma_start(out=mem_v[:, 4 * h : 4 * h + 4, :], in_=mem_rows[:, 4 * h : 4 * h + 4, :])
+        cur_sb = []
+        for k in range(CHUNKS):
+            cur_k = keep.tile([P, CHUNK * D], BF16, name="cur%d" % k)
+            nc.sync.dma_start(out=cur_k[:], in_=cur_rows[:, k * CHUNK * D : (k + 1) * CHUNK * D])
+            cur_sb.append(cur_k)
+
+        ident = keep.tile([P, P], F32)
+        make_identity(nc, ident[:])
+        ident_bf = keep.tile([P, P], BF16)
+        make_identity(nc, ident_bf[:])
+        one = keep.tile([P, 1], F32)
+        nc.vector.memset(one[:], 1.0)
+        warm = keep.tile([P, 1], F32)
+        nc.scalar.activation(out=warm[:], in_=one[:], func=FN.Sqrt)
+
+        def words_out(engine_is_vector, dst_words, bank):
+            src = bank[:].rearrange("q (i u b) -> q i b u", i=2, u=2)
+            dst = dst_words.rearrange("q (i b u) -> q i b u", i=2, u=2)
+            if engine_is_vector:
+                nc.vector.tensor_copy(out=dst, in_=src)
+            else:
+                nc.scalar.copy(out=dst, in_=src)
+
+        mem_w = mem_sb[:].bitcast(F32)
+        g_m = keep.tile([P, 4 * C], BF16, align_bytes=64)
+        g_m_w = g_m[:].bitcast(F32)
+        m_codes = keep.tile([P, C], U32, align_bytes=64)
+        m_scales = keep.tile([P, C], U8, align_bytes=64)
+        for jp in range(4):
+            bank = ps_tr.tile([P, 512], F32, tag="tr")
+            for n in range(4):
+                nc.tensor.transpose(bank[:, n * P : (n + 1) * P], mem_w[:, 512 * jp + P * n : 512 * jp + P * (n + 1)], ident[:])
+            words_out(True, g_m_w[:, 512 * jp : 512 * (jp + 1)], bank)
+            if jp % 2 == 1:
+                h = jp // 2
+                nc.vector.quantize_mx(
+                    out=m_codes[:, 512 * h : 512 * (h + 1)].bitcast(FP8X4),
+                    scales=m_scales[:, 512 * h : 512 * (h + 1)],
+                    in_=g_m[:, 2048 * h : 2048 * (h + 1)],
+                )
+
+        m_ss = keep.tile([P, 8], F32)
+        for j in range(8):
+            junk = junkp.tile([P, D], BF16)
+            nc.scalar.activation(out=junk[:], in_=mem_v[:, j, :], func=FN.Square, accum_out=m_ss[:, j : j + 1])
+        m_cl = keep.tile([P, 8], F32)
+        nc.vector.tensor_scalar_max(out=m_cl[:], in0=m_ss[:], scalar1=EPS * EPS)
+        m_n = keep.tile([P, 8], F32)
+        nc.scalar.activation(out=m_n[:], in_=m_cl[:], func=FN.Sqrt)
+        m_r = keep.tile([P, 8], F32)
+        nc.vector.reciprocal(out=m_r[:], in_=m_n[:])
+        r_all = keep.tile([P, C], F32)
+        for h in range(2):
+            bank = ps_sim.tile([P, 512], F32, tag="sim")
+            for n in range(4):
+                j = 4 * h + n
+                nc.tensor.matmul(
+                    out=bank[:, n * P : (n + 1) * P],
+                    lhsT=m_r[:, j : j + 1].to_broadcast([P, P]),
+                    rhs=ident[:],
+                    start=True,
+                    stop=True,
+                )
+            nc.vector.tensor_copy(out=r_all[:, 512 * h : 512 * (h + 1)], in_=bank[:])
+
+        c_codes = []
+        c_scales = []
+
+        def prepare_current(k):
+            cw = cur_sb[k][:].bitcast(F32)
+            g_c = gcp.tile([P, CHUNK * D], BF16, align_bytes=64)
+            g_c_w = g_c[:].bitcast(F32)
+            for pr in range(2):
+                bank = ps_tr.tile([P, 512], F32, tag="tr")
+                for n in range(4):
+                    nc.tensor.transpose(bank[:, n * P : (n + 1) * P], cw[:, 512 * pr + P * n : 512 * pr + P * (n + 1)], ident[:])
+                words_out(k in CURCOPY_ON_VECTOR, g_c_w[:, 512 * pr : 512 * (pr + 1)], bank)
+            codes = keep.tile([P, CHUNK * P], U32, name="c_codes%d" % k, align_bytes=64)
+            scales = keep.tile([P, CHUNK * P], U8, name="c_scales%d" % k, align_bytes=64)
+            nc.vector.quantize_mx(out=codes[:].bitcast(FP8X4), scales=scales[:], in_=g_c[:])
+            c_codes.append(codes)
+            c_scales.append(scales)
+
+        prepare_current(0)
+        prepare_current(1)
+
+        k_codes = keep.tile([P, 2 * D], U32, align_bytes=64)
+        k_scales = keep.tile([P, 2 * D], U8, align_bytes=64)
+        for g in range(2):
+            g_k = keep.tile([P, 4 * D], BF16, name="g_k%d" % g, align_bytes=64)
+            nc.vector.tensor_copy(
+                out=g_k[:].rearrange("p (c i t) -> p c t i", i=4, t=4),
+                in_=mem_sb[:, 2048 * g : 2048 * (g + 1)].rearrange("p (t c i) -> p c t i", t=4, i=4),
+            )
+            nc.vector.quantize_mx(
+                out=k_codes[:, D * g : D * (g + 1)].bitcast(FP8X4),
+                scales=k_scales[:, D * g : D * (g + 1)],
+                in_=g_k[:],
+            )
+
+        c_ss = keep.tile([P, TILES], F32)
+        for t in range(TILES):
+            k, i = divmod(t, CHUNK)
+            junk = junkp.tile([P, D], BF16)
+            nc.scalar.activation(out=junk[:], in_=cur_sb[k][:, D * i : D * (i + 1)], func=FN.Square, accum_out=c_ss[:, t : t + 1])
+        c_cl = keep.tile([P, TILES], F32)
+        nc.vector.tensor_scalar_max(out=c_cl[:], in0=c_ss[:], scalar1=EPS * EPS)
+        c_n = keep.tile([P, TILES], F32)
+        nc.scalar.activation(out=c_n[:], in_=c_cl[:], func=FN.Sqrt)
+        a_all = keep.tile([P, TILES], F32)
+        nc.vector.reciprocal(out=a_all[:], in_=c_n[:])
+
+        ys = {}
+        nbs = {}
+        es = {}
+        sums = {}
+        ecs = {}
+        c02s = {}
+        outs = {}
+
+        def similarity(t):
+            k, i = divmod(t, CHUNK)
+            y = yp.tile([P, C], F32)
+            for h in range(2):
+                ps = ps_sim.tile([P, 512], F32, tag="sim")
+                nc.tensor.matmul_mx(
+                    out=ps[:],
+                    lhsT=c_codes[k][:, P * i : P * (i + 1)].bitcast(FP8X4),
+                    lhsT_scale=c_scales[k][:, P * i : P * (i + 1)],
+                    rhs=m_codes[:, 512 * h : 512 * (h + 1)].bitcast(FP8X4),
+                    rhs_scale=m_scales[:, 512 * h : 512 * (h + 1)],
+                    start=True,
+                    stop=True,
+                )
+                nc.vector.tensor_tensor(out=y[:, 512 * h : 512 * (h + 1)], in0=ps[:], in1=r_all[:, 512 * h : 512 * (h + 1)], op=ALU.mult)
+            top = small.tile([P, 1], F32)
+            nc.vector.tensor_reduce(out=top[:], in_=y[:], axis=AXIS_X, op=ALU.max)
+            nb = small.tile([P, 1], F32)
+            nc.vector.tensor_scalar(out=nb[:], in0=top[:], scalar1=a_all[:, t : t + 1], scalar2=-1.0, op0=ALU.mult, op1=ALU.mult)
+            ys[t] = y
+            nbs[t] = nb
+
+        def exponent(t):
+            e = ep.tile([P, C], BF16)
+            rs = small.tile([P, 1], F32)
+            nc.scalar.activation(out=e[:], in_=ys[t][:], func=FN.Exp, bias=nbs[t][:], scale=a_all[:, t : t + 1], accum_out=rs[:])
+            es[t] = e
+            sums[t] = rs
+
+        def transpose_e(t):
+            bank = ps_tr.tile([P, C], BF16, tag="tr")
+            for n in range(8):
+                nc.tensor.transpose(bank[:, n * P : (n + 1) * P], es[t][:, n * P : (n + 1) * P], ident_bf[:])
+            g_e = ep.tile([P, C], BF16, align_bytes=64)
+            dst = g_e[:].rearrange("p (g b t) -> p g b t", g=2, t=4)
+            src = bank[:].rearrange("p (g t b) -> p g b t", g=2, t=4)
+            if t in C1_ON_VECTOR:
+                nc.vector.tensor_copy(out=dst, in_=src)
+            else:
+                nc.scalar.copy(out=dst, in_=src)
+            e_codes = ep.tile([P, 2 * P], U32, align_bytes=64)
+            e_scales = ep.tile([P, 2 * P], U8, align_bytes=64)
+            nc.vector.quantize_mx(out=e_codes[:].bitcast(FP8X4), scales=e_scales[:], in_=g_e[:])
+            ecs[t] = (e_codes, e_scales)
+
+        def attract(t):
+            k, i = divmod(t, CHUNK)
+            e_codes, e_scales = ecs[t]
+            acc = ps_acc.tile([P, D], F32)
+            for g in range(2):
+                nc.tensor.matmul_mx(
+                    out=acc[:],
+                    lhsT=e_codes[:, P * g : P * (g + 1)].bitcast(FP8X4),
+                    lhsT_scale=e_scales[:, P * g : P * (g + 1)],
+                    rhs=k_codes[:, D * g : D * (g + 1)].bitcast(FP8X4),
+                    rhs_scale=k_scales[:, D * g : D * (g + 1)],
+                    start=(g == 0),
+                    stop=(g == 1),
+                )
+            big = small.tile([P, 1], F32)
+            nc.vector.tensor_scalar_mul(out=big[:], in0=sums[t][:], scalar1=1.25)
+            sc = small.tile([P, 1], F32)
+            nc.vector.reciprocal(out=sc[:], in_=big[:])
+            if t % 2 == 0:
+                o = op.tile([P, 2 * D], F32)
+                outs[t // 2] = o
+            o = outs[t // 2]
+            half = o[:, D * (t % 2) : D * (t % 2 + 1)]
+            nc.vector.scalar_tensor_tensor(out=half, in0=acc[:], scalar=sc[:], in1=c02s[k][:, D * i : D * (i + 1)], op0=ALU.mult, op1=ALU.add)
+            if t % 2 == 1:
+                nc.sync.dma_start(out=out_rows[:, D * (t - 1) : D * (t + 1)], in_=o[:])
+
+        for n in range(TILES + 3):
+            if n % CHUNK == 0 and n // CHUNK + 2 < CHUNKS:
+                prepare_current(n // CHUNK + 2)
+            if n % CHUNK == 0 and n // CHUNK < CHUNKS:
+                k = n // CHUNK
+                c02 = c02p.tile([P, CHUNK * D], F32)
+                nc.gpsimd.tensor_scalar(out=c02[:], in0=cur_sb[k][:], scalar1=0.2, scalar2=0.0, op0=ALU.mult, op1=ALU.add)
+                c02s[k] = c02
+            if n < TILES:
+                similarity(n)
+            if 0 <= n - 1 < TILES:
+                exponent(n - 1)
+            if 0 <= n - 2 < TILES:
+                transpose_e(n - 2)
+            if 0 <= n - 3 < TILES:
+                attract(n - 3)

@@ -20,8 +20,8 @@ CHUNKS = TILES // CHUNK
 EPS = 1e-8
 FLOPS = 2 * B * C * D * 2
 
-E1_ON_VECTOR = True
-CURCOPY_ON_VECTOR = (0, 1, 2)
+HEAD_TILES = 6
+CURCOPY_ON_VECTOR = (0, 1)
 C1_ON_VECTOR = ()
 
 
@@ -35,11 +35,10 @@ def tile_ca3_recurrentmatrix_pa_t_kernel(tc, current, memory_matrix, out):
         keep = stack.enter_context(tc.tile_pool(name="keep", bufs=1))
         junkp = stack.enter_context(tc.tile_pool(name="junkp", bufs=2))
         gcp = stack.enter_context(tc.tile_pool(name="gcp", bufs=2))
-        yp = stack.enter_context(tc.tile_pool(name="yp", bufs=6))
+        yp = stack.enter_context(tc.tile_pool(name="yp", bufs=7))
         ep = stack.enter_context(tc.tile_pool(name="ep", bufs=3))
         small = stack.enter_context(tc.tile_pool(name="small", bufs=8))
-        c02p = stack.enter_context(tc.tile_pool(name="c02p", bufs=3))
-        op = stack.enter_context(tc.tile_pool(name="op", bufs=3))
+        op = stack.enter_context(tc.tile_pool(name="op", bufs=2))
         ps_sim = stack.enter_context(tc.psum_pool(name="ps_sim", bufs=4))
         ps_tr = stack.enter_context(tc.psum_pool(name="ps_tr", bufs=2))
         ps_acc = stack.enter_context(tc.psum_pool(name="ps_acc", bufs=2))
@@ -62,6 +61,15 @@ def tile_ca3_recurrentmatrix_pa_t_kernel(tc, current, memory_matrix, out):
         nc.vector.memset(one[:], 1.0)
         warm = keep.tile([P, 1], F32)
         nc.scalar.activation(out=warm[:], in_=one[:], func=FN.Sqrt)
+
+        c02s = []
+        for k in range(CHUNKS):
+            c02 = keep.tile([P, CHUNK * D], F32, name="c02_%d" % k)
+            for i in range(CHUNK):
+                nc.gpsimd.tensor_scalar(
+                    out=c02[:, D * i : D * (i + 1)], in0=cur_sb[k][:, D * i : D * (i + 1)], scalar1=0.2, scalar2=0.0, op0=ALU.mult, op1=ALU.add
+                )
+            c02s.append(c02)
 
         def words_out(engine_is_vector, dst_words, bank):
             src = bank[:].rearrange("q (i u b) -> q i b u", i=2, u=2)
@@ -159,14 +167,17 @@ def tile_ca3_recurrentmatrix_pa_t_kernel(tc, current, memory_matrix, out):
         nc.scalar.activation(out=c_n[:], in_=c_cl[:], func=FN.Sqrt)
         a_all = keep.tile([P, TILES], F32)
         nc.vector.reciprocal(out=a_all[:], in_=c_n[:])
+        na_all = keep.tile([P, TILES], F32)
+        nc.vector.tensor_scalar_mul(out=na_all[:], in0=a_all[:], scalar1=-1.0)
 
         ys = {}
         nbs = {}
         es = {}
         sums = {}
         ecs = {}
-        c02s = {}
+        ges = {}
         outs = {}
+        scs = {}
 
         def similarity(t):
             k, i = divmod(t, CHUNK)
@@ -182,77 +193,92 @@ def tile_ca3_recurrentmatrix_pa_t_kernel(tc, current, memory_matrix, out):
                     start=True,
                     stop=True,
                 )
-                nc.vector.tensor_tensor(out=y[:, 512 * h : 512 * (h + 1)], in0=ps[:], in1=r_all[:, 512 * h : 512 * (h + 1)], op=ALU.mult)
-            top = small.tile([P, 1], F32)
-            nc.vector.tensor_reduce(out=top[:], in_=y[:], axis=AXIS_X, op=ALU.max)
+                if t < HEAD_TILES:
+                    nc.vector.tensor_tensor(out=y[:, 512 * h : 512 * (h + 1)], in0=ps[:], in1=r_all[:, 512 * h : 512 * (h + 1)], op=ALU.mult)
+                else:
+                    nc.vector.scalar_tensor_tensor(
+                        out=y[:, 512 * h : 512 * (h + 1)], in0=ps[:], scalar=na_all[:, t : t + 1], in1=r_all[:, 512 * h : 512 * (h + 1)], op0=ALU.mult, op1=ALU.mult
+                    )
             nb = small.tile([P, 1], F32)
-            nc.vector.tensor_scalar(out=nb[:], in0=top[:], scalar1=a_all[:, t : t + 1], scalar2=-1.0, op0=ALU.mult, op1=ALU.mult)
+            if t < HEAD_TILES:
+                top = small.tile([P, 1], F32)
+                nc.vector.tensor_reduce(out=top[:], in_=y[:], axis=AXIS_X, op=ALU.max)
+                nc.vector.tensor_scalar_mul(out=nb[:], in0=top[:], scalar1=na_all[:, t : t + 1])
+            else:
+                nc.vector.tensor_reduce(out=nb[:], in_=y[:], axis=AXIS_X, op=ALU.min)
             ys[t] = y
             nbs[t] = nb
 
         def exponent(t):
             e = ep.tile([P, C], BF16)
-            rs = small.tile([P, 1], F32)
-            nc.scalar.activation(out=e[:], in_=ys[t][:], func=FN.Exp, bias=nbs[t][:], scale=a_all[:, t : t + 1], accum_out=rs[:])
+            if t % 2 == 0:
+                rs = small.tile([P, 2], F32)
+                sums[t // 2] = rs
+            rs_col = sums[t // 2][:, t % 2 : t % 2 + 1]
+            if t < HEAD_TILES:
+                nc.scalar.activation(out=e[:], in_=ys[t][:], func=FN.Exp, bias=nbs[t][:], scale=a_all[:, t : t + 1], accum_out=rs_col)
+            else:
+                nc.scalar.activation(out=e[:], in_=ys[t][:], func=FN.Exp, bias=nbs[t][:], scale=-1.0, accum_out=rs_col)
             es[t] = e
-            sums[t] = rs
 
         def transpose_e(t):
             bank = ps_tr.tile([P, C], BF16, tag="tr")
             for n in range(8):
                 nc.tensor.transpose(bank[:, n * P : (n + 1) * P], es[t][:, n * P : (n + 1) * P], ident_bf[:])
-            g_e = ep.tile([P, C], BF16, align_bytes=64)
-            dst = g_e[:].rearrange("p (g b t) -> p g b t", g=2, t=4)
+            if t % 2 == 0:
+                g_e = ep.tile([P, 2 * C], BF16, align_bytes=64)
+                ges[t // 2] = g_e
+            dst = ges[t // 2][:, C * (t % 2) : C * (t % 2 + 1)].rearrange("p (g b t) -> p g b t", g=2, t=4)
             src = bank[:].rearrange("p (g t b) -> p g b t", g=2, t=4)
             if t in C1_ON_VECTOR:
                 nc.vector.tensor_copy(out=dst, in_=src)
             else:
                 nc.scalar.copy(out=dst, in_=src)
-            e_codes = ep.tile([P, 2 * P], U32, align_bytes=64)
-            e_scales = ep.tile([P, 2 * P], U8, align_bytes=64)
-            nc.vector.quantize_mx(out=e_codes[:].bitcast(FP8X4), scales=e_scales[:], in_=g_e[:])
-            ecs[t] = (e_codes, e_scales)
+            if t % 2 == 1:
+                e_codes = ep.tile([P, 4 * P], U32, align_bytes=64)
+                e_scales = ep.tile([P, 4 * P], U8, align_bytes=64)
+                nc.vector.quantize_mx(out=e_codes[:].bitcast(FP8X4), scales=e_scales[:], in_=ges[t // 2][:])
+                ecs[t // 2] = (e_codes, e_scales)
 
         def attract(t):
             k, i = divmod(t, CHUNK)
-            e_codes, e_scales = ecs[t]
+            e_codes, e_scales = ecs[t // 2]
             acc = ps_acc.tile([P, D], F32)
             for g in range(2):
+                w = 2 * (t % 2) + g
                 nc.tensor.matmul_mx(
                     out=acc[:],
-                    lhsT=e_codes[:, P * g : P * (g + 1)].bitcast(FP8X4),
-                    lhsT_scale=e_scales[:, P * g : P * (g + 1)],
+                    lhsT=e_codes[:, P * w : P * (w + 1)].bitcast(FP8X4),
+                    lhsT_scale=e_scales[:, P * w : P * (w + 1)],
                     rhs=k_codes[:, D * g : D * (g + 1)].bitcast(FP8X4),
                     rhs_scale=k_scales[:, D * g : D * (g + 1)],
                     start=(g == 0),
                     stop=(g == 1),
                 )
-            big = small.tile([P, 1], F32)
-            nc.vector.tensor_scalar_mul(out=big[:], in0=sums[t][:], scalar1=1.25)
-            sc = small.tile([P, 1], F32)
-            nc.vector.reciprocal(out=sc[:], in_=big[:])
             if t % 2 == 0:
+                big = small.tile([P, 2], F32)
+                nc.vector.tensor_scalar_mul(out=big[:], in0=sums[t // 2][:], scalar1=1.25)
+                sc2 = small.tile([P, 2], F32)
+                nc.vector.reciprocal(out=sc2[:], in_=big[:])
+                scs[t // 2] = sc2
                 o = op.tile([P, 2 * D], F32)
                 outs[t // 2] = o
             o = outs[t // 2]
+            sc = scs[t // 2][:, t % 2 : t % 2 + 1]
             half = o[:, D * (t % 2) : D * (t % 2 + 1)]
-            nc.vector.scalar_tensor_tensor(out=half, in0=acc[:], scalar=sc[:], in1=c02s[k][:, D * i : D * (i + 1)], op0=ALU.mult, op1=ALU.add)
+            nc.vector.scalar_tensor_tensor(out=half, in0=acc[:], scalar=sc, in1=c02s[k][:, D * i : D * (i + 1)], op0=ALU.mult, op1=ALU.add)
             if t % 2 == 1:
                 nc.sync.dma_start(out=out_rows[:, D * (t - 1) : D * (t + 1)], in_=o[:])
 
-        for n in range(TILES + 3):
+        for n in range(TILES + 5):
             if n % CHUNK == 0 and n // CHUNK + 2 < CHUNKS:
                 prepare_current(n // CHUNK + 2)
-            if n % CHUNK == 0 and n // CHUNK < CHUNKS:
-                k = n // CHUNK
-                c02 = c02p.tile([P, CHUNK * D], F32)
-                nc.gpsimd.tensor_scalar(out=c02[:], in0=cur_sb[k][:], scalar1=0.2, scalar2=0.0, op0=ALU.mult, op1=ALU.add)
-                c02s[k] = c02
             if n < TILES:
                 similarity(n)
             if 0 <= n - 1 < TILES:
                 exponent(n - 1)
             if 0 <= n - 2 < TILES:
                 transpose_e(n - 2)
-            if 0 <= n - 3 < TILES:
-                attract(n - 3)
+            if n % 2 == 1 and 0 <= n - 5 < TILES:
+                attract(n - 5)
+                attract(n - 4)

@@ -21,6 +21,7 @@ EPS = 1e-8
 FLOPS = 2 * B * C * D * 2
 
 HEAD_TILES = 6
+SIM_PASSES = 2
 CURCOPY_ON_VECTOR = (0, 1)
 C1_ON_VECTOR = ()
 
@@ -184,15 +185,16 @@ def tile_ca3_recurrentmatrix_pa_t_kernel(tc, current, memory_matrix, out):
             y = yp.tile([P, C], F32)
             for h in range(2):
                 ps = ps_sim.tile([P, 512], F32, tag="sim")
-                nc.tensor.matmul_mx(
-                    out=ps[:],
-                    lhsT=c_codes[k][:, P * i : P * (i + 1)].bitcast(FP8X4),
-                    lhsT_scale=c_scales[k][:, P * i : P * (i + 1)],
-                    rhs=m_codes[:, 512 * h : 512 * (h + 1)].bitcast(FP8X4),
-                    rhs_scale=m_scales[:, 512 * h : 512 * (h + 1)],
-                    start=True,
-                    stop=True,
-                )
+                for again in range(SIM_PASSES):
+                    nc.tensor.matmul_mx(
+                        out=ps[:],
+                        lhsT=c_codes[k][:, P * i : P * (i + 1)].bitcast(FP8X4),
+                        lhsT_scale=c_scales[k][:, P * i : P * (i + 1)],
+                        rhs=m_codes[:, 512 * h : 512 * (h + 1)].bitcast(FP8X4),
+                        rhs_scale=m_scales[:, 512 * h : 512 * (h + 1)],
+                        start=True,
+                        stop=True,
+                    )
                 if t < HEAD_TILES:
                     nc.vector.tensor_tensor(out=y[:, 512 * h : 512 * (h + 1)], in0=ps[:], in1=r_all[:, 512 * h : 512 * (h + 1)], op=ALU.mult)
                 else:

@@ -20,10 +20,8 @@ CHUNKS = TILES // CHUNK
 EPS = 1e-8
 FLOPS = 2 * B * C * D * 2
 
-HEAD_TILES = 6
 SIM_PASSES = 2
-CURCOPY_ON_VECTOR = (0, 1)
-C1_ON_VECTOR = ()
+ON_SCALAR = (0, 1)
 
 
 def tile_ca3_recurrentmatrix_pa_t_kernel(tc, current, memory_matrix, out):
@@ -36,10 +34,11 @@ def tile_ca3_recurrentmatrix_pa_t_kernel(tc, current, memory_matrix, out):
         keep = stack.enter_context(tc.tile_pool(name="keep", bufs=1))
         junkp = stack.enter_context(tc.tile_pool(name="junkp", bufs=2))
         gcp = stack.enter_context(tc.tile_pool(name="gcp", bufs=2))
-        yp = stack.enter_context(tc.tile_pool(name="yp", bufs=7))
+        c02p = stack.enter_context(tc.tile_pool(name="c02p", bufs=4))
+        yp = stack.enter_context(tc.tile_pool(name="yp", bufs=5))
         ep = stack.enter_context(tc.tile_pool(name="ep", bufs=3))
         small = stack.enter_context(tc.tile_pool(name="small", bufs=8))
-        op = stack.enter_context(tc.tile_pool(name="op", bufs=2))
+        op = stack.enter_context(tc.tile_pool(name="op", bufs=3))
         ps_sim = stack.enter_context(tc.psum_pool(name="ps_sim", bufs=4))
         ps_tr = stack.enter_context(tc.psum_pool(name="ps_tr", bufs=2))
         ps_acc = stack.enter_context(tc.psum_pool(name="ps_acc", bufs=2))
@@ -56,29 +55,28 @@ def tile_ca3_recurrentmatrix_pa_t_kernel(tc, current, memory_matrix, out):
 
         ident = keep.tile([P, P], F32)
         make_identity(nc, ident[:])
-        ident_bf = keep.tile([P, P], BF16)
-        make_identity(nc, ident_bf[:])
         one = keep.tile([P, 1], F32)
         nc.vector.memset(one[:], 1.0)
+        minus_half = keep.tile([P, 8], F32)
+        nc.vector.memset(minus_half[:], -0.5)
         warm = keep.tile([P, 1], F32)
-        nc.scalar.activation(out=warm[:], in_=one[:], func=FN.Sqrt)
+        nc.scalar.activation(out=warm[:], in_=one[:], func=FN.Exp)
 
-        c02s = []
-        for k in range(CHUNKS):
-            c02 = keep.tile([P, CHUNK * D], F32, name="c02_%d" % k)
-            for i in range(CHUNK):
-                nc.gpsimd.tensor_scalar(
-                    out=c02[:, D * i : D * (i + 1)], in0=cur_sb[k][:, D * i : D * (i + 1)], scalar1=0.2, scalar2=0.0, op0=ALU.mult, op1=ALU.add
-                )
-            c02s.append(c02)
+        def sum_squares(dst, row):
+            junk = junkp.tile([P, D], BF16)
+            nc.scalar.activation(out=junk[:], in_=row, func=FN.Square, accum_out=dst)
 
-        def words_out(engine_is_vector, dst_words, bank):
-            src = bank[:].rearrange("q (i u b) -> q i b u", i=2, u=2)
-            dst = dst_words.rearrange("q (i b u) -> q i b u", i=2, u=2)
-            if engine_is_vector:
-                nc.vector.tensor_copy(out=dst, in_=src)
-            else:
-                nc.scalar.copy(out=dst, in_=src)
+        def inverse_norms(ss, n, name):
+            floor = keep.tile([P, n], F32, name="floor_" + name)
+            nc.gpsimd.tensor_scalar(out=floor[:], in0=ss, scalar1=EPS * EPS, scalar2=1.0, op0=ALU.max, op1=ALU.mult)
+            inv = keep.tile([P, n], F32, name="inv_" + name)
+            nc.gpsimd.tensor_tensor(out=inv[:], in0=floor[:], in1=minus_half[:, 0:n], op=ALU.pow)
+            return inv
+
+        m_ss = keep.tile([P, 8], F32)
+        for j in range(8):
+            sum_squares(m_ss[:, j : j + 1], mem_v[:, j, :])
+        m_r = inverse_norms(m_ss[:], 8, "m")
 
         mem_w = mem_sb[:].bitcast(F32)
         g_m = keep.tile([P, 4 * C], BF16, align_bytes=64)
@@ -89,7 +87,10 @@ def tile_ca3_recurrentmatrix_pa_t_kernel(tc, current, memory_matrix, out):
             bank = ps_tr.tile([P, 512], F32, tag="tr")
             for n in range(4):
                 nc.tensor.transpose(bank[:, n * P : (n + 1) * P], mem_w[:, 512 * jp + P * n : 512 * jp + P * (n + 1)], ident[:])
-            words_out(True, g_m_w[:, 512 * jp : 512 * (jp + 1)], bank)
+            nc.vector.tensor_copy(
+                out=g_m_w[:, 512 * jp : 512 * (jp + 1)].rearrange("q (b i u) -> q b i u", i=2, u=2),
+                in_=bank[:].rearrange("q (i u b) -> q b i u", i=2, u=2),
+            )
             if jp % 2 == 1:
                 h = jp // 2
                 nc.vector.quantize_mx(
@@ -98,17 +99,42 @@ def tile_ca3_recurrentmatrix_pa_t_kernel(tc, current, memory_matrix, out):
                     in_=g_m[:, 2048 * h : 2048 * (h + 1)],
                 )
 
-        m_ss = keep.tile([P, 8], F32)
-        for j in range(8):
-            junk = junkp.tile([P, D], BF16)
-            nc.scalar.activation(out=junk[:], in_=mem_v[:, j, :], func=FN.Square, accum_out=m_ss[:, j : j + 1])
-        m_cl = keep.tile([P, 8], F32)
-        nc.vector.tensor_scalar_max(out=m_cl[:], in0=m_ss[:], scalar1=EPS * EPS)
-        m_n = keep.tile([P, 8], F32)
-        nc.scalar.activation(out=m_n[:], in_=m_cl[:], func=FN.Sqrt)
-        m_r = keep.tile([P, 8], F32)
-        nc.vector.reciprocal(out=m_r[:], in_=m_n[:])
-        r_all = keep.tile([P, C], F32)
+        c_codes = []
+        c_scales = []
+        c_inv = []
+        c02s = []
+
+        def prepare_current(k):
+            cw = cur_sb[k][:].bitcast(F32)
+            g_c = gcp.tile([P, CHUNK * D], BF16, align_bytes=64)
+            g_c_w = g_c[:].bitcast(F32)
+            for pr in range(2):
+                bank = ps_tr.tile([P, 512], F32, tag="tr")
+                for n in range(4):
+                    nc.tensor.transpose(bank[:, n * P : (n + 1) * P], cw[:, 512 * pr + P * n : 512 * pr + P * (n + 1)], ident[:])
+                nc.scalar.copy(
+                    out=g_c_w[:, 512 * pr : 512 * (pr + 1)].rearrange("q (i b u) -> q i b u", i=2, u=2),
+                    in_=bank[:].rearrange("q (i u b) -> q i b u", i=2, u=2),
+                )
+            codes = keep.tile([P, CHUNK * P], U32, name="c_codes%d" % k, align_bytes=64)
+            scales = keep.tile([P, CHUNK * P], U8, name="c_scales%d" % k, align_bytes=64)
+            nc.vector.quantize_mx(out=codes[:].bitcast(FP8X4), scales=scales[:], in_=g_c[:])
+            c_codes.append(codes)
+            c_scales.append(scales)
+            ss = keep.tile([P, CHUNK], F32, name="c_ss%d" % k)
+            for i in range(CHUNK):
+                sum_squares(ss[:, i : i + 1], cur_sb[k][:, D * i : D * (i + 1)])
+            c_inv.append(inverse_norms(ss[:], CHUNK, "c%d" % k))
+            c02 = c02p.tile([P, CHUNK * D], F32)
+            for i in range(CHUNK):
+                nc.gpsimd.tensor_scalar(
+                    out=c02[:, D * i : D * (i + 1)], in0=cur_sb[k][:, D * i : D * (i + 1)], scalar1=0.2, scalar2=0.0, op0=ALU.mult, op1=ALU.add
+                )
+            c02s.append(c02)
+
+        prepare_current(0)
+
+        r_neg = keep.tile([P, C], F32)
         for h in range(2):
             bank = ps_sim.tile([P, 512], F32, tag="sim")
             for n in range(4):
@@ -120,28 +146,11 @@ def tile_ca3_recurrentmatrix_pa_t_kernel(tc, current, memory_matrix, out):
                     start=True,
                     stop=True,
                 )
-            nc.vector.tensor_copy(out=r_all[:, 512 * h : 512 * (h + 1)], in_=bank[:])
-
-        c_codes = []
-        c_scales = []
-
-        def prepare_current(k):
-            cw = cur_sb[k][:].bitcast(F32)
-            g_c = gcp.tile([P, CHUNK * D], BF16, align_bytes=64)
-            g_c_w = g_c[:].bitcast(F32)
-            for pr in range(2):
-                bank = ps_tr.tile([P, 512], F32, tag="tr")
-                for n in range(4):
-                    nc.tensor.transpose(bank[:, n * P : (n + 1) * P], cw[:, 512 * pr + P * n : 512 * pr + P * (n + 1)], ident[:])
-                words_out(k in CURCOPY_ON_VECTOR, g_c_w[:, 512 * pr : 512 * (pr + 1)], bank)
-            codes = keep.tile([P, CHUNK * P], U32, name="c_codes%d" % k, align_bytes=64)
-            scales = keep.tile([P, CHUNK * P], U8, name="c_scales%d" % k, align_bytes=64)
-            nc.vector.quantize_mx(out=codes[:].bitcast(FP8X4), scales=scales[:], in_=g_c[:])
-            c_codes.append(codes)
-            c_scales.append(scales)
-
-        prepare_current(0)
-        prepare_current(1)
+            nc.vector.tensor_scalar_mul(
+                out=r_neg[:, 512 * h : 512 * (h + 1)].rearrange("q (m b i) -> q m b i", m=2, i=2),
+                in0=bank[:].rearrange("q (m i b) -> q m b i", m=2, i=2),
+                scalar1=-1.0,
+            )
 
         k_codes = keep.tile([P, 2 * D], U32, align_bytes=64)
         k_scales = keep.tile([P, 2 * D], U8, align_bytes=64)
@@ -157,19 +166,7 @@ def tile_ca3_recurrentmatrix_pa_t_kernel(tc, current, memory_matrix, out):
                 in_=g_k[:],
             )
 
-        c_ss = keep.tile([P, TILES], F32)
-        for t in range(TILES):
-            k, i = divmod(t, CHUNK)
-            junk = junkp.tile([P, D], BF16)
-            nc.scalar.activation(out=junk[:], in_=cur_sb[k][:, D * i : D * (i + 1)], func=FN.Square, accum_out=c_ss[:, t : t + 1])
-        c_cl = keep.tile([P, TILES], F32)
-        nc.vector.tensor_scalar_max(out=c_cl[:], in0=c_ss[:], scalar1=EPS * EPS)
-        c_n = keep.tile([P, TILES], F32)
-        nc.scalar.activation(out=c_n[:], in_=c_cl[:], func=FN.Sqrt)
-        a_all = keep.tile([P, TILES], F32)
-        nc.vector.reciprocal(out=a_all[:], in_=c_n[:])
-        na_all = keep.tile([P, TILES], F32)
-        nc.vector.tensor_scalar_mul(out=na_all[:], in0=a_all[:], scalar1=-1.0)
+        prepare_current(1)
 
         ys = {}
         nbs = {}
@@ -195,19 +192,11 @@ def tile_ca3_recurrentmatrix_pa_t_kernel(tc, current, memory_matrix, out):
                         start=True,
                         stop=True,
                     )
-                if t < HEAD_TILES:
-                    nc.vector.tensor_tensor(out=y[:, 512 * h : 512 * (h + 1)], in0=ps[:], in1=r_all[:, 512 * h : 512 * (h + 1)], op=ALU.mult)
-                else:
-                    nc.vector.scalar_tensor_tensor(
-                        out=y[:, 512 * h : 512 * (h + 1)], in0=ps[:], scalar=na_all[:, t : t + 1], in1=r_all[:, 512 * h : 512 * (h + 1)], op0=ALU.mult, op1=ALU.mult
-                    )
+                nc.vector.scalar_tensor_tensor(
+                    out=y[:, 512 * h : 512 * (h + 1)], in0=ps[:], scalar=c_inv[k][:, i : i + 1], in1=r_neg[:, 512 * h : 512 * (h + 1)], op0=ALU.mult, op1=ALU.mult
+                )
             nb = small.tile([P, 1], F32)
-            if t < HEAD_TILES:
-                top = small.tile([P, 1], F32)
-                nc.vector.tensor_reduce(out=top[:], in_=y[:], axis=AXIS_X, op=ALU.max)
-                nc.vector.tensor_scalar_mul(out=nb[:], in0=top[:], scalar1=na_all[:, t : t + 1])
-            else:
-                nc.vector.tensor_reduce(out=nb[:], in_=y[:], axis=AXIS_X, op=ALU.min)
+            nc.vector.tensor_reduce(out=nb[:], in_=y[:], axis=AXIS_X, op=ALU.min)
             ys[t] = y
             nbs[t] = nb
 
@@ -217,25 +206,20 @@ def tile_ca3_recurrentmatrix_pa_t_kernel(tc, current, memory_matrix, out):
                 rs = small.tile([P, 2], F32)
                 sums[t // 2] = rs
             rs_col = sums[t // 2][:, t % 2 : t % 2 + 1]
-            if t < HEAD_TILES:
-                nc.scalar.activation(out=e[:], in_=ys[t][:], func=FN.Exp, bias=nbs[t][:], scale=a_all[:, t : t + 1], accum_out=rs_col)
-            else:
-                nc.scalar.activation(out=e[:], in_=ys[t][:], func=FN.Exp, bias=nbs[t][:], scale=-1.0, accum_out=rs_col)
+            nc.scalar.activation(out=e[:], in_=ys[t][:], func=FN.Exp, bias=nbs[t][:], scale=-1.0, accum_out=rs_col)
             es[t] = e
 
         def transpose_e(t):
-            bank = ps_tr.tile([P, C], BF16, tag="tr")
-            for n in range(8):
-                nc.tensor.transpose(bank[:, n * P : (n + 1) * P], es[t][:, n * P : (n + 1) * P], ident_bf[:])
+            bank = ps_tr.tile([P, 512], F32, tag="tr")
+            e_w = es[t][:].bitcast(F32)
+            for n in range(4):
+                nc.tensor.transpose(bank[:, n * P : (n + 1) * P], e_w[:, n * P : (n + 1) * P], ident[:])
             if t % 2 == 0:
                 g_e = ep.tile([P, 2 * C], BF16, align_bytes=64)
                 ges[t // 2] = g_e
-            dst = ges[t // 2][:, C * (t % 2) : C * (t % 2 + 1)].rearrange("p (g b t) -> p g b t", g=2, t=4)
-            src = bank[:].rearrange("p (g t b) -> p g b t", g=2, t=4)
-            if t in C1_ON_VECTOR:
-                nc.vector.tensor_copy(out=dst, in_=src)
-            else:
-                nc.scalar.copy(out=dst, in_=src)
+            dst = ges[t // 2][:].bitcast(F32)[:, 512 * (t % 2) : 512 * (t % 2 + 1)].rearrange("p (g b u) -> p g b u", g=2, u=2)
+            src = bank[:].rearrange("p (g u b) -> p g b u", g=2, u=2)
+            nc.scalar.copy(out=dst, in_=src)
             if t % 2 == 1:
                 e_codes = ep.tile([P, 4 * P], U32, align_bytes=64)
                 e_scales = ep.tile([P, 4 * P], U8, align_bytes=64)
@@ -268,7 +252,12 @@ def tile_ca3_recurrentmatrix_pa_t_kernel(tc, current, memory_matrix, out):
             o = outs[t // 2]
             sc = scs[t // 2][:, t % 2 : t % 2 + 1]
             half = o[:, D * (t % 2) : D * (t % 2 + 1)]
-            nc.vector.scalar_tensor_tensor(out=half, in0=acc[:], scalar=sc, in1=c02s[k][:, D * i : D * (i + 1)], op0=ALU.mult, op1=ALU.add)
+            fifth = c02s[k][:, D * i : D * (i + 1)]
+            if t % 3 in ON_SCALAR:
+                nc.scalar.activation(out=half, in_=acc[:], func=FN.Copy, scale=sc)
+                nc.gpsimd.tensor_tensor(out=half, in0=half, in1=fifth, op=ALU.add)
+            else:
+                nc.vector.scalar_tensor_tensor(out=half, in0=acc[:], scalar=sc, in1=fifth, op0=ALU.mult, op1=ALU.add)
             if t % 2 == 1:
                 nc.sync.dma_start(out=out_rows[:, D * (t - 1) : D * (t + 1)], in_=o[:])
 

@@ -20,9 +20,6 @@ CHUNKS = TILES // CHUNK
 EPS = 1e-8
 FLOPS = 2 * B * C * D * 2
 
-SIM_PASSES = 2
-ON_SCALAR = (0, 1)
-
 
 def tile_ca3_recurrentmatrix_pa_t_kernel(tc, current, memory_matrix, out):
     nc = tc.nc
@@ -34,19 +31,20 @@ def tile_ca3_recurrentmatrix_pa_t_kernel(tc, current, memory_matrix, out):
         keep = stack.enter_context(tc.tile_pool(name="keep", bufs=1))
         junkp = stack.enter_context(tc.tile_pool(name="junkp", bufs=2))
         gcp = stack.enter_context(tc.tile_pool(name="gcp", bufs=2))
-        c02p = stack.enter_context(tc.tile_pool(name="c02p", bufs=4))
-        yp = stack.enter_context(tc.tile_pool(name="yp", bufs=5))
+        c02p = stack.enter_context(tc.tile_pool(name="c02p", bufs=8))
+        yp = stack.enter_context(tc.tile_pool(name="yp", bufs=4))
         ep = stack.enter_context(tc.tile_pool(name="ep", bufs=3))
         small = stack.enter_context(tc.tile_pool(name="small", bufs=8))
-        op = stack.enter_context(tc.tile_pool(name="op", bufs=3))
+        op = stack.enter_context(tc.tile_pool(name="op", bufs=4))
         ps_sim = stack.enter_context(tc.psum_pool(name="ps_sim", bufs=4))
         ps_tr = stack.enter_context(tc.psum_pool(name="ps_tr", bufs=2))
         ps_acc = stack.enter_context(tc.psum_pool(name="ps_acc", bufs=2))
+        stack.enter_context(tc.manual_schedule())
 
         mem_sb = keep.tile([P, 8 * D], BF16)
         mem_v = mem_sb[:].rearrange("p (j d) -> p j d", j=8)
-        for h in range(2):
-            nc.sync.dma_start(out=mem_v[:, 4 * h : 4 * h + 4, :], in_=mem_rows[:, 4 * h : 4 * h + 4, :])
+        for h in range(4):
+            nc.sync.dma_start(out=mem_v[:, 2 * h : 2 * h + 2, :], in_=mem_rows[:, 2 * h : 2 * h + 2, :])
         cur_sb = []
         for k in range(CHUNKS):
             cur_k = keep.tile([P, CHUNK * D], BF16, name="cur%d" % k)
@@ -73,203 +71,326 @@ def tile_ca3_recurrentmatrix_pa_t_kernel(tc, current, memory_matrix, out):
             nc.gpsimd.tensor_tensor(out=inv[:], in0=floor[:], in1=minus_half[:, 0:n], op=ALU.pow)
             return inv
 
-        m_ss = keep.tile([P, 8], F32)
-        for j in range(8):
-            sum_squares(m_ss[:, j : j + 1], mem_v[:, j, :])
-        m_r = inverse_norms(m_ss[:], 8, "m")
+        g_cs = {}
+        c_banks = {}
+        c_codes = {}
+        c_scales = {}
+        c_ss = {}
+        c_inv = {}
+
+        def turn_current(k, pr):
+            if pr == 0:
+                g_c = gcp.tile([P, CHUNK * D], BF16, align_bytes=64)
+                g_cs[k] = g_c
+            cw = cur_sb[k][:].bitcast(F32)
+            bank = ps_tr.tile([P, 512], F32, tag="tr")
+            for n in range(4):
+                nc.tensor.transpose(bank[:, n * P : (n + 1) * P], cw[:, 512 * pr + P * n : 512 * pr + P * (n + 1)], ident[:])
+            c_banks[k, pr] = bank
+
+        def regroup_current(k, pr):
+            bank = c_banks[k, pr]
+            nc.scalar.copy(
+                out=g_cs[k][:].bitcast(F32)[:, 512 * pr : 512 * (pr + 1)].rearrange("q (i b u) -> q i b u", i=2, u=2),
+                in_=bank[:].rearrange("q (i u b) -> q i b u", i=2, u=2),
+            )
+
+        def quantise_current(k):
+            codes = keep.tile([P, CHUNK * P], U32, name="c_codes%d" % k, align_bytes=64)
+            scales = keep.tile([P, CHUNK * P], U8, name="c_scales%d" % k, align_bytes=64)
+            nc.vector.quantize_mx(out=codes[:].bitcast(FP8X4), scales=scales[:], in_=g_cs[k][:])
+            c_codes[k] = codes
+            c_scales[k] = scales
+
+        def square_current(k, i):
+            if i == 0:
+                ss = keep.tile([P, CHUNK], F32, name="c_ss%d" % k)
+                c_ss[k] = ss
+            sum_squares(c_ss[k][:, i : i + 1], cur_sb[k][:, D * i : D * (i + 1)])
+            if i == CHUNK - 1:
+                c_inv[k] = inverse_norms(c_ss[k][:], CHUNK, "c%d" % k)
 
         mem_w = mem_sb[:].bitcast(F32)
+        m_ss = []
+        m_r = []
+        for h in range(2):
+            ss = keep.tile([P, 4], F32, name="m_ss%d" % h)
+            m_ss.append(ss)
         g_m = keep.tile([P, 4 * C], BF16, align_bytes=64)
-        g_m_w = g_m[:].bitcast(F32)
         m_codes = keep.tile([P, C], U32, align_bytes=64)
         m_scales = keep.tile([P, C], U8, align_bytes=64)
-        for jp in range(4):
-            bank = ps_tr.tile([P, 512], F32, tag="tr")
+        k_codes = keep.tile([P, 2 * D], U32, align_bytes=64)
+        k_scales = keep.tile([P, 2 * D], U8, align_bytes=64)
+        g_k = []
+        for g in range(2):
+            g_kg = keep.tile([P, 4 * D], BF16, name="g_k%d" % g, align_bytes=64)
+            g_k.append(g_kg)
+        r_neg = keep.tile([P, C], F32)
+
+        def square_memory(h):
+            for j in range(4):
+                row = mem_v[:, 4 * h + j, :]
+                if h == 0:
+                    sum_squares(m_ss[h][:, j : j + 1], row)
+                else:
+                    junk = junkp.tile([P, D], BF16, name="vjunk")
+                    nc.vector.scalar_tensor_tensor(
+                        out=junk[:], in0=row, scalar=1.0, in1=row, op0=ALU.mult, op1=ALU.mult, accum_out=m_ss[h][:, j : j + 1]
+                    )
+            m_r.append(inverse_norms(m_ss[h][:], 4, "m%d" % h))
+
+        def turn_memory(jp):
+            bank = ps_sim.tile([P, 512], F32, tag="sim")
             for n in range(4):
                 nc.tensor.transpose(bank[:, n * P : (n + 1) * P], mem_w[:, 512 * jp + P * n : 512 * jp + P * (n + 1)], ident[:])
             nc.vector.tensor_copy(
-                out=g_m_w[:, 512 * jp : 512 * (jp + 1)].rearrange("q (b i u) -> q b i u", i=2, u=2),
+                out=g_m[:].bitcast(F32)[:, 512 * jp : 512 * (jp + 1)].rearrange("q (b i u) -> q b i u", i=2, u=2),
                 in_=bank[:].rearrange("q (i u b) -> q b i u", i=2, u=2),
             )
-            if jp % 2 == 1:
-                h = jp // 2
-                nc.vector.quantize_mx(
-                    out=m_codes[:, 512 * h : 512 * (h + 1)].bitcast(FP8X4),
-                    scales=m_scales[:, 512 * h : 512 * (h + 1)],
-                    in_=g_m[:, 2048 * h : 2048 * (h + 1)],
-                )
 
-        c_codes = []
-        c_scales = []
-        c_inv = []
-        c02s = []
+        def quantise_memory(h):
+            nc.vector.quantize_mx(
+                out=m_codes[:, 512 * h : 512 * (h + 1)].bitcast(FP8X4),
+                scales=m_scales[:, 512 * h : 512 * (h + 1)],
+                in_=g_m[:, 2048 * h : 2048 * (h + 1)],
+            )
 
-        def prepare_current(k):
-            cw = cur_sb[k][:].bitcast(F32)
-            g_c = gcp.tile([P, CHUNK * D], BF16, align_bytes=64)
-            g_c_w = g_c[:].bitcast(F32)
-            for pr in range(2):
-                bank = ps_tr.tile([P, 512], F32, tag="tr")
-                for n in range(4):
-                    nc.tensor.transpose(bank[:, n * P : (n + 1) * P], cw[:, 512 * pr + P * n : 512 * pr + P * (n + 1)], ident[:])
-                nc.scalar.copy(
-                    out=g_c_w[:, 512 * pr : 512 * (pr + 1)].rearrange("q (i b u) -> q i b u", i=2, u=2),
-                    in_=bank[:].rearrange("q (i u b) -> q i b u", i=2, u=2),
-                )
-            codes = keep.tile([P, CHUNK * P], U32, name="c_codes%d" % k, align_bytes=64)
-            scales = keep.tile([P, CHUNK * P], U8, name="c_scales%d" % k, align_bytes=64)
-            nc.vector.quantize_mx(out=codes[:].bitcast(FP8X4), scales=scales[:], in_=g_c[:])
-            c_codes.append(codes)
-            c_scales.append(scales)
-            ss = keep.tile([P, CHUNK], F32, name="c_ss%d" % k)
-            for i in range(CHUNK):
-                sum_squares(ss[:, i : i + 1], cur_sb[k][:, D * i : D * (i + 1)])
-            c_inv.append(inverse_norms(ss[:], CHUNK, "c%d" % k))
-            c02 = c02p.tile([P, CHUNK * D], F32)
-            for i in range(CHUNK):
-                nc.gpsimd.tensor_scalar(
-                    out=c02[:, D * i : D * (i + 1)], in0=cur_sb[k][:, D * i : D * (i + 1)], scalar1=0.2, scalar2=0.0, op0=ALU.mult, op1=ALU.add
-                )
-            c02s.append(c02)
+        def regroup_memory(g):
+            nc.gpsimd.tensor_scalar(
+                out=g_k[g][:].rearrange("p (c i t) -> p c t i", i=4, t=4),
+                in0=mem_sb[:, 2048 * g : 2048 * (g + 1)].rearrange("p (t c i) -> p c t i", t=4, i=4),
+                scalar1=1.0,
+                scalar2=0.0,
+                op0=ALU.mult,
+                op1=ALU.add,
+            )
 
-        prepare_current(0)
+        def quantise_rows(g):
+            nc.vector.quantize_mx(
+                out=k_codes[:, D * g : D * (g + 1)].bitcast(FP8X4),
+                scales=k_scales[:, D * g : D * (g + 1)],
+                in_=g_k[g][:],
+            )
 
-        r_neg = keep.tile([P, C], F32)
-        for h in range(2):
+        r_banks = []
+
+        def spread_norms(h):
             bank = ps_sim.tile([P, 512], F32, tag="sim")
             for n in range(4):
-                j = 4 * h + n
                 nc.tensor.matmul(
                     out=bank[:, n * P : (n + 1) * P],
-                    lhsT=m_r[:, j : j + 1].to_broadcast([P, P]),
+                    lhsT=m_r[h][:, n : n + 1].to_broadcast([P, P]),
                     rhs=ident[:],
                     start=True,
                     stop=True,
                 )
+            r_banks.append(bank)
+
+        def keep_norms(h):
             nc.vector.tensor_scalar_mul(
                 out=r_neg[:, 512 * h : 512 * (h + 1)].rearrange("q (m b i) -> q m b i", m=2, i=2),
-                in0=bank[:].rearrange("q (m i b) -> q m b i", m=2, i=2),
+                in0=r_banks[h][:].rearrange("q (m i b) -> q m b i", m=2, i=2),
                 scalar1=-1.0,
             )
 
-        k_codes = keep.tile([P, 2 * D], U32, align_bytes=64)
-        k_scales = keep.tile([P, 2 * D], U8, align_bytes=64)
+        square_memory(0)
+        turn_memory(0)
+        turn_memory(1)
+        square_memory(1)
+        turn_memory(2)
+        turn_memory(3)
+        for pr in range(2):
+            turn_current(0, pr)
+            regroup_current(0, pr)
+        for i in range(CHUNK):
+            square_current(0, i)
+        quantise_memory(0)
+        quantise_current(0)
+        quantise_memory(1)
+        spread_norms(0)
+        for pr in range(2):
+            turn_current(1, pr)
+            regroup_current(1, pr)
+        spread_norms(1)
+        keep_norms(0)
+        keep_norms(1)
         for g in range(2):
-            g_k = keep.tile([P, 4 * D], BF16, name="g_k%d" % g, align_bytes=64)
-            nc.vector.tensor_copy(
-                out=g_k[:].rearrange("p (c i t) -> p c t i", i=4, t=4),
-                in_=mem_sb[:, 2048 * g : 2048 * (g + 1)].rearrange("p (t c i) -> p c t i", t=4, i=4),
-            )
-            nc.vector.quantize_mx(
-                out=k_codes[:, D * g : D * (g + 1)].bitcast(FP8X4),
-                scales=k_scales[:, D * g : D * (g + 1)],
-                in_=g_k[:],
-            )
+            regroup_memory(g)
+        for i in range(CHUNK):
+            square_current(1, i)
 
-        prepare_current(1)
-
+        sim_banks = {}
         ys = {}
         nbs = {}
         es = {}
-        sums = {}
-        ecs = {}
+        rss = {}
+        e_banks = {}
         ges = {}
-        outs = {}
+        ecs = {}
+        accs = {}
         scs = {}
+        bigs = {}
+        fifths = {}
+        outs = {}
 
-        def similarity(t):
+        def multiply_similarity(t):
             k, i = divmod(t, CHUNK)
-            y = yp.tile([P, C], F32)
             for h in range(2):
                 ps = ps_sim.tile([P, 512], F32, tag="sim")
-                for again in range(SIM_PASSES):
-                    nc.tensor.matmul_mx(
-                        out=ps[:],
-                        lhsT=c_codes[k][:, P * i : P * (i + 1)].bitcast(FP8X4),
-                        lhsT_scale=c_scales[k][:, P * i : P * (i + 1)],
-                        rhs=m_codes[:, 512 * h : 512 * (h + 1)].bitcast(FP8X4),
-                        rhs_scale=m_scales[:, 512 * h : 512 * (h + 1)],
-                        start=True,
-                        stop=True,
-                    )
-                nc.vector.scalar_tensor_tensor(
-                    out=y[:, 512 * h : 512 * (h + 1)], in0=ps[:], scalar=c_inv[k][:, i : i + 1], in1=r_neg[:, 512 * h : 512 * (h + 1)], op0=ALU.mult, op1=ALU.mult
+                nc.tensor.matmul_mx(
+                    out=ps[:],
+                    lhsT=c_codes[k][:, P * i : P * (i + 1)].bitcast(FP8X4),
+                    lhsT_scale=c_scales[k][:, P * i : P * (i + 1)],
+                    rhs=m_codes[:, 512 * h : 512 * (h + 1)].bitcast(FP8X4),
+                    rhs_scale=m_scales[:, 512 * h : 512 * (h + 1)],
+                    start=True,
+                    stop=True,
                 )
-            nb = small.tile([P, 1], F32)
-            nc.vector.tensor_reduce(out=nb[:], in_=y[:], axis=AXIS_X, op=ALU.min)
+                sim_banks[t, h] = ps
+
+        def scale_similarity(t):
+            k, i = divmod(t, CHUNK)
+            y = yp.tile([P, C], F32)
             ys[t] = y
+            for h in range(2):
+                nc.vector.scalar_tensor_tensor(
+                    out=y[:, 512 * h : 512 * (h + 1)],
+                    in0=sim_banks[t, h][:],
+                    scalar=c_inv[k][:, i : i + 1],
+                    in1=r_neg[:, 512 * h : 512 * (h + 1)],
+                    op0=ALU.mult,
+                    op1=ALU.mult,
+                )
+
+        def find_maximum(t):
+            nb = small.tile([P, 1], F32)
+            nc.vector.tensor_reduce(out=nb[:], in_=ys[t][:], axis=AXIS_X, op=ALU.min)
             nbs[t] = nb
 
         def exponent(t):
             e = ep.tile([P, C], BF16)
-            if t % 2 == 0:
-                rs = small.tile([P, 2], F32)
-                sums[t // 2] = rs
-            rs_col = sums[t // 2][:, t % 2 : t % 2 + 1]
-            nc.scalar.activation(out=e[:], in_=ys[t][:], func=FN.Exp, bias=nbs[t][:], scale=-1.0, accum_out=rs_col)
+            rs = small.tile([P, 1], F32)
+            nc.scalar.activation(out=e[:], in_=ys[t][:], func=FN.Exp, bias=nbs[t][:], scale=-1.0, accum_out=rs[:])
             es[t] = e
+            rss[t] = rs
 
         def transpose_e(t):
             bank = ps_tr.tile([P, 512], F32, tag="tr")
             e_w = es[t][:].bitcast(F32)
             for n in range(4):
                 nc.tensor.transpose(bank[:, n * P : (n + 1) * P], e_w[:, n * P : (n + 1) * P], ident[:])
-            if t % 2 == 0:
-                g_e = ep.tile([P, 2 * C], BF16, align_bytes=64)
-                ges[t // 2] = g_e
-            dst = ges[t // 2][:].bitcast(F32)[:, 512 * (t % 2) : 512 * (t % 2 + 1)].rearrange("p (g b u) -> p g b u", g=2, u=2)
-            src = bank[:].rearrange("p (g u b) -> p g b u", g=2, u=2)
-            nc.scalar.copy(out=dst, in_=src)
-            if t % 2 == 1:
-                e_codes = ep.tile([P, 4 * P], U32, align_bytes=64)
-                e_scales = ep.tile([P, 4 * P], U8, align_bytes=64)
-                nc.vector.quantize_mx(out=e_codes[:].bitcast(FP8X4), scales=e_scales[:], in_=ges[t // 2][:])
-                ecs[t // 2] = (e_codes, e_scales)
+            e_banks[t] = bank
 
-        def attract(t):
+        def regroup_e(t):
+            g_e = ep.tile([P, C], BF16, align_bytes=64)
+            nc.scalar.copy(
+                out=g_e[:].bitcast(F32).rearrange("p (g b u) -> p g b u", g=2, u=2),
+                in_=e_banks[t][:].rearrange("p (g u b) -> p g b u", g=2, u=2),
+            )
+            ges[t] = g_e
+
+        def quantise_e(t):
+            e_codes = ep.tile([P, 2 * P], U32, align_bytes=64)
+            e_scales = ep.tile([P, 2 * P], U8, align_bytes=64)
+            nc.vector.quantize_mx(out=e_codes[:].bitcast(FP8X4), scales=e_scales[:], in_=ges[t][:])
+            ecs[t] = (e_codes, e_scales)
+
+        def weigh(t):
+            big = small.tile([P, 1], F32)
+            nc.gpsimd.tensor_scalar(out=big[:], in0=rss[t][:], scalar1=1.25, scalar2=0.0, op0=ALU.mult, op1=ALU.add)
+            bigs[t] = big
+
+        def invert_weight(t):
+            sc = small.tile([P, 1], F32)
+            nc.vector.reciprocal(out=sc[:], in_=bigs[t][:])
+            scs[t] = sc
+
+        def fifth(t):
             k, i = divmod(t, CHUNK)
-            e_codes, e_scales = ecs[t // 2]
+            c02 = c02p.tile([P, D], F32)
+            nc.gpsimd.tensor_scalar(out=c02[:], in0=cur_sb[k][:, D * i : D * (i + 1)], scalar1=0.2, scalar2=0.0, op0=ALU.mult, op1=ALU.add)
+            fifths[t] = c02
+
+        def multiply_attracted(t):
+            e_codes, e_scales = ecs[t]
             acc = ps_acc.tile([P, D], F32)
             for g in range(2):
-                w = 2 * (t % 2) + g
                 nc.tensor.matmul_mx(
                     out=acc[:],
-                    lhsT=e_codes[:, P * w : P * (w + 1)].bitcast(FP8X4),
-                    lhsT_scale=e_scales[:, P * w : P * (w + 1)],
+                    lhsT=e_codes[:, P * g : P * (g + 1)].bitcast(FP8X4),
+                    lhsT_scale=e_scales[:, P * g : P * (g + 1)],
                     rhs=k_codes[:, D * g : D * (g + 1)].bitcast(FP8X4),
                     rhs_scale=k_scales[:, D * g : D * (g + 1)],
                     start=(g == 0),
                     stop=(g == 1),
                 )
+            accs[t] = acc
+
+        def on_scalar(t):
+            return t < 27 and t % 3 != 2
+
+        def output_half(t):
             if t % 2 == 0:
-                big = small.tile([P, 2], F32)
-                nc.vector.tensor_scalar_mul(out=big[:], in0=sums[t // 2][:], scalar1=1.25)
-                sc2 = small.tile([P, 2], F32)
-                nc.vector.reciprocal(out=sc2[:], in_=big[:])
-                scs[t // 2] = sc2
                 o = op.tile([P, 2 * D], F32)
                 outs[t // 2] = o
-            o = outs[t // 2]
-            sc = scs[t // 2][:, t % 2 : t % 2 + 1]
-            half = o[:, D * (t % 2) : D * (t % 2 + 1)]
-            fifth = c02s[k][:, D * i : D * (i + 1)]
-            if t % 3 in ON_SCALAR:
-                nc.scalar.activation(out=half, in_=acc[:], func=FN.Copy, scale=sc)
-                nc.gpsimd.tensor_tensor(out=half, in0=half, in1=fifth, op=ALU.add)
-            else:
-                nc.vector.scalar_tensor_tensor(out=half, in0=acc[:], scalar=sc, in1=fifth, op0=ALU.mult, op1=ALU.add)
-            if t % 2 == 1:
-                nc.sync.dma_start(out=out_rows[:, D * (t - 1) : D * (t + 1)], in_=o[:])
+            return outs[t // 2][:, D * (t % 2) : D * (t % 2 + 1)]
 
-        for n in range(TILES + 5):
-            if n % CHUNK == 0 and n // CHUNK + 2 < CHUNKS:
-                prepare_current(n // CHUNK + 2)
-            if n < TILES:
-                similarity(n)
-            if 0 <= n - 1 < TILES:
-                exponent(n - 1)
-            if 0 <= n - 2 < TILES:
+        def finish_on_scalar(t):
+            half = output_half(t)
+            nc.scalar.activation(out=half, in_=accs[t][:], func=FN.Copy, scale=scs[t][:])
+            nc.gpsimd.tensor_tensor(out=half, in0=half, in1=fifths[t][:], op=ALU.add)
+
+        def finish_on_vector(t):
+            half = output_half(t)
+            nc.vector.scalar_tensor_tensor(out=half, in0=accs[t][:], scalar=scs[t][:], in1=fifths[t][:], op0=ALU.mult, op1=ALU.add)
+
+        def store(t):
+            if t % 2 == 1:
+                nc.sync.dma_start(out=out_rows[:, D * (t - 1) : D * (t + 1)], in_=outs[t // 2][:])
+
+        def live(t):
+            return 0 <= t < TILES
+
+        multiply_similarity(0)
+        for n in range(TILES + 6):
+            k, q = divmod(n, CHUNK)
+            more = 1 <= k and k + 1 < CHUNKS
+            if more and q < 2:
+                turn_current(k + 1, q)
+            if live(n - 2):
                 transpose_e(n - 2)
-            if n % 2 == 1 and 0 <= n - 5 < TILES:
-                attract(n - 5)
-                attract(n - 4)
+            if live(n + 1):
+                multiply_similarity(n + 1)
+            if live(n - 4):
+                multiply_attracted(n - 4)
+            if live(n - 5) and on_scalar(n - 5):
+                finish_on_scalar(n - 5)
+            if more:
+                for i in ((0,), (1,), (2, 3), ())[q]:
+                    square_current(k + 1, i)
+            if more and q < 2:
+                regroup_current(k + 1, q)
+            if live(n):
+                scale_similarity(n)
+            if live(n - 3):
+                quantise_e(n - 3)
+                invert_weight(n - 3)
+            if live(n):
+                find_maximum(n)
+            if n == 1:
+                quantise_current(1)
+            if n in (2, 3):
+                quantise_rows(n - 2)
+            if more and q == 2:
+                quantise_current(k + 1)
+            if live(n - 5) and not on_scalar(n - 5):
+                finish_on_vector(n - 5)
+            if live(n - 5):
+                store(n - 5)
+            if live(n):
+                fifth(n)
+            if live(n - 1):
+                exponent(n - 1)
+                weigh(n - 1)
+            if live(n - 2):
+                regroup_e(n - 2)

@@ -18,6 +18,7 @@ TILES = B // P
 CHUNK = 4
 CHUNKS = TILES // CHUNK
 EPS = 1e-8
+PREP_SLOTS = 26
 FLOPS = 2 * B * C * D * 2
 
 
@@ -31,10 +32,11 @@ def tile_ca3_recurrentmatrix_pa_t_kernel(tc, current, memory_matrix, out):
         keep = stack.enter_context(tc.tile_pool(name="keep", bufs=1))
         junkp = stack.enter_context(tc.tile_pool(name="junkp", bufs=2))
         gcp = stack.enter_context(tc.tile_pool(name="gcp", bufs=2))
-        c02p = stack.enter_context(tc.tile_pool(name="c02p", bufs=8))
+        c02p = stack.enter_context(tc.tile_pool(name="c02p", bufs=11))
         yp = stack.enter_context(tc.tile_pool(name="yp", bufs=4))
         ep = stack.enter_context(tc.tile_pool(name="ep", bufs=3))
-        small = stack.enter_context(tc.tile_pool(name="small", bufs=8))
+        small = stack.enter_context(tc.tile_pool(name="small", bufs=10))
+        gep = stack.enter_context(tc.tile_pool(name="gep", bufs=2))
         op = stack.enter_context(tc.tile_pool(name="op", bufs=4))
         ps_sim = stack.enter_context(tc.psum_pool(name="ps_sim", bufs=4))
         ps_tr = stack.enter_context(tc.psum_pool(name="ps_tr", bufs=2))
@@ -103,12 +105,13 @@ def tile_ca3_recurrentmatrix_pa_t_kernel(tc, current, memory_matrix, out):
             c_scales[k] = scales
 
         def square_current(k, i):
-            if i == 0:
-                ss = keep.tile([P, CHUNK], F32, name="c_ss%d" % k)
-                c_ss[k] = ss
-            sum_squares(c_ss[k][:, i : i + 1], cur_sb[k][:, D * i : D * (i + 1)])
-            if i == CHUNK - 1:
-                c_inv[k] = inverse_norms(c_ss[k][:], CHUNK, "c%d" % k)
+            pair, s = divmod(i, 2)
+            if s == 0:
+                ss = keep.tile([P, 2], F32, name="c_ss%d_%d" % (k, pair))
+                c_ss[k, pair] = ss
+            sum_squares(c_ss[k, pair][:, s : s + 1], cur_sb[k][:, D * i : D * (i + 1)])
+            if s == 1:
+                c_inv[k, pair] = inverse_norms(c_ss[k, pair][:], 2, "c%d_%d" % (k, pair))
 
         mem_w = mem_sb[:].bitcast(F32)
         m_ss = []
@@ -143,10 +146,12 @@ def tile_ca3_recurrentmatrix_pa_t_kernel(tc, current, memory_matrix, out):
             bank = ps_sim.tile([P, 512], F32, tag="sim")
             for n in range(4):
                 nc.tensor.transpose(bank[:, n * P : (n + 1) * P], mem_w[:, 512 * jp + P * n : 512 * jp + P * (n + 1)], ident[:])
-            nc.vector.tensor_copy(
-                out=g_m[:].bitcast(F32)[:, 512 * jp : 512 * (jp + 1)].rearrange("q (b i u) -> q b i u", i=2, u=2),
-                in_=bank[:].rearrange("q (i u b) -> q b i u", i=2, u=2),
-            )
+            dst = g_m[:].bitcast(F32)[:, 512 * jp : 512 * (jp + 1)].rearrange("q (b i u) -> q b i u", i=2, u=2)
+            src = bank[:].rearrange("q (i u b) -> q b i u", i=2, u=2)
+            if jp < 2:
+                nc.vector.tensor_copy(out=dst, in_=src)
+            else:
+                nc.scalar.copy(out=dst, in_=src)
 
         def quantise_memory(h):
             nc.vector.quantize_mx(
@@ -177,13 +182,7 @@ def tile_ca3_recurrentmatrix_pa_t_kernel(tc, current, memory_matrix, out):
         def spread_norms(h):
             bank = ps_sim.tile([P, 512], F32, tag="sim")
             for n in range(4):
-                nc.tensor.matmul(
-                    out=bank[:, n * P : (n + 1) * P],
-                    lhsT=m_r[h][:, n : n + 1].to_broadcast([P, P]),
-                    rhs=ident[:],
-                    start=True,
-                    stop=True,
-                )
+                nc.tensor.transpose(bank[:, n * P : (n + 1) * P], m_r[h][:, n : n + 1].to_broadcast([P, P]), ident[:])
             r_banks.append(bank)
 
         def keep_norms(h):
@@ -256,7 +255,7 @@ def tile_ca3_recurrentmatrix_pa_t_kernel(tc, current, memory_matrix, out):
                 nc.vector.scalar_tensor_tensor(
                     out=y[:, 512 * h : 512 * (h + 1)],
                     in0=sim_banks[t, h][:],
-                    scalar=c_inv[k][:, i : i + 1],
+                    scalar=c_inv[k, i // 2][:, i % 2 : i % 2 + 1],
                     in1=r_neg[:, 512 * h : 512 * (h + 1)],
                     op0=ALU.mult,
                     op1=ALU.mult,
@@ -269,10 +268,13 @@ def tile_ca3_recurrentmatrix_pa_t_kernel(tc, current, memory_matrix, out):
 
         def exponent(t):
             e = ep.tile([P, C], BF16)
-            rs = small.tile([P, 1], F32)
-            nc.scalar.activation(out=e[:], in_=ys[t][:], func=FN.Exp, bias=nbs[t][:], scale=-1.0, accum_out=rs[:])
+            if t % 2 == 0:
+                rs = small.tile([P, 2], F32)
+                rss[t // 2] = rs
+            nc.scalar.activation(
+                out=e[:], in_=ys[t][:], func=FN.Exp, bias=nbs[t][:], scale=-1.0, accum_out=rss[t // 2][:, t % 2 : t % 2 + 1]
+            )
             es[t] = e
-            rss[t] = rs
 
         def transpose_e(t):
             bank = ps_tr.tile([P, 512], F32, tag="tr")
@@ -282,28 +284,36 @@ def tile_ca3_recurrentmatrix_pa_t_kernel(tc, current, memory_matrix, out):
             e_banks[t] = bank
 
         def regroup_e(t):
-            g_e = ep.tile([P, C], BF16, align_bytes=64)
+            k, i = divmod(t, CHUNK)
+            if i == 0:
+                g_e = gep.tile([P, CHUNK * C], BF16, align_bytes=64)
+                ges[k] = g_e
             nc.scalar.copy(
-                out=g_e[:].bitcast(F32).rearrange("p (g b u) -> p g b u", g=2, u=2),
+                out=ges[k][:].bitcast(F32)[:, 512 * i : 512 * (i + 1)].rearrange("p (g b u) -> p g b u", g=2, u=2),
                 in_=e_banks[t][:].rearrange("p (g u b) -> p g b u", g=2, u=2),
             )
-            ges[t] = g_e
 
-        def quantise_e(t):
-            e_codes = ep.tile([P, 2 * P], U32, align_bytes=64)
-            e_scales = ep.tile([P, 2 * P], U8, align_bytes=64)
-            nc.vector.quantize_mx(out=e_codes[:].bitcast(FP8X4), scales=e_scales[:], in_=ges[t][:])
-            ecs[t] = (e_codes, e_scales)
+        def quantise_e(t, tiles):
+            k, i = divmod(t, CHUNK)
+            if k not in ecs:
+                e_codes = gep.tile([P, CHUNK * 2 * P], U32, align_bytes=64)
+                e_scales = gep.tile([P, CHUNK * 2 * P], U8, align_bytes=64)
+                ecs[k] = (e_codes, e_scales)
+            e_codes, e_scales = ecs[k]
+            words = slice(2 * P * i, 2 * P * (i + tiles))
+            nc.vector.quantize_mx(out=e_codes[:, words].bitcast(FP8X4), scales=e_scales[:, words], in_=ges[k][:, C * i : C * (i + tiles)])
 
         def weigh(t):
-            big = small.tile([P, 1], F32)
-            nc.gpsimd.tensor_scalar(out=big[:], in0=rss[t][:], scalar1=1.25, scalar2=0.0, op0=ALU.mult, op1=ALU.add)
-            bigs[t] = big
+            if t % 2 == 1:
+                big = small.tile([P, 2], F32)
+                nc.gpsimd.tensor_scalar(out=big[:], in0=rss[t // 2][:], scalar1=1.25, scalar2=0.0, op0=ALU.mult, op1=ALU.add)
+                bigs[t // 2] = big
 
         def invert_weight(t):
-            sc = small.tile([P, 1], F32)
-            nc.vector.reciprocal(out=sc[:], in_=bigs[t][:])
-            scs[t] = sc
+            if t % 2 == 1:
+                sc = small.tile([P, 2], F32)
+                nc.vector.reciprocal(out=sc[:], in_=bigs[t // 2][:])
+                scs[t // 2] = sc
 
         def fifth(t):
             k, i = divmod(t, CHUNK)
@@ -312,13 +322,14 @@ def tile_ca3_recurrentmatrix_pa_t_kernel(tc, current, memory_matrix, out):
             fifths[t] = c02
 
         def multiply_attracted(t):
-            e_codes, e_scales = ecs[t]
+            e_codes, e_scales = ecs[t // CHUNK]
             acc = ps_acc.tile([P, D], F32)
             for g in range(2):
+                w = 2 * (t % CHUNK) + g
                 nc.tensor.matmul_mx(
                     out=acc[:],
-                    lhsT=e_codes[:, P * g : P * (g + 1)].bitcast(FP8X4),
-                    lhsT_scale=e_scales[:, P * g : P * (g + 1)],
+                    lhsT=e_codes[:, P * w : P * (w + 1)].bitcast(FP8X4),
+                    lhsT_scale=e_scales[:, P * w : P * (w + 1)],
                     rhs=k_codes[:, D * g : D * (g + 1)].bitcast(FP8X4),
                     rhs_scale=k_scales[:, D * g : D * (g + 1)],
                     start=(g == 0),
@@ -327,7 +338,7 @@ def tile_ca3_recurrentmatrix_pa_t_kernel(tc, current, memory_matrix, out):
             accs[t] = acc
 
         def on_scalar(t):
-            return t < 27 and t % 3 != 2
+            return t < 27 and t % 6 != 2
 
         def output_half(t):
             if t % 2 == 0:
@@ -337,12 +348,12 @@ def tile_ca3_recurrentmatrix_pa_t_kernel(tc, current, memory_matrix, out):
 
         def finish_on_scalar(t):
             half = output_half(t)
-            nc.scalar.activation(out=half, in_=accs[t][:], func=FN.Copy, scale=scs[t][:])
+            nc.scalar.activation(out=half, in_=accs[t][:], func=FN.Copy, scale=scs[t // 2][:, t % 2 : t % 2 + 1])
             nc.gpsimd.tensor_tensor(out=half, in0=half, in1=fifths[t][:], op=ALU.add)
 
         def finish_on_vector(t):
             half = output_half(t)
-            nc.vector.scalar_tensor_tensor(out=half, in0=accs[t][:], scalar=scs[t][:], in1=fifths[t][:], op0=ALU.mult, op1=ALU.add)
+            nc.vector.scalar_tensor_tensor(out=half, in0=accs[t][:], scalar=scs[t // 2][:, t % 2 : t % 2 + 1], in1=fifths[t][:], op0=ALU.mult, op1=ALU.add)
 
         def store(t):
             if t % 2 == 1:
@@ -351,46 +362,54 @@ def tile_ca3_recurrentmatrix_pa_t_kernel(tc, current, memory_matrix, out):
         def live(t):
             return 0 <= t < TILES
 
+        pieces = []
+        for k in range(2, CHUNKS):
+            pieces += [(regroup_current, k, 0), (regroup_current, k, 1)] + [(square_current, k, i) for i in range(CHUNK)]
+        done = 0
         multiply_similarity(0)
-        for n in range(TILES + 6):
-            k, q = divmod(n, CHUNK)
-            more = 1 <= k and k + 1 < CHUNKS
-            if more and q < 2:
-                turn_current(k + 1, q)
+        for n in range(TILES + 7):
+            now = pieces[done : (n + 1) * len(pieces) // PREP_SLOTS]
+            done += len(now)
+            later = pieces[done : (n + 2) * len(pieces) // PREP_SLOTS]
             if live(n - 2):
                 transpose_e(n - 2)
             if live(n + 1):
                 multiply_similarity(n + 1)
-            if live(n - 4):
-                multiply_attracted(n - 4)
-            if live(n - 5) and on_scalar(n - 5):
-                finish_on_scalar(n - 5)
-            if more:
-                for i in ((0,), (1,), (2, 3), ())[q]:
-                    square_current(k + 1, i)
-            if more and q < 2:
-                regroup_current(k + 1, q)
+            for stage, k, i in (now + later if n == 0 else later):
+                if stage == regroup_current:
+                    turn_current(k, i)
+            if live(n - 6) and on_scalar(n - 6):
+                finish_on_scalar(n - 6)
+            for stage, k, i in now:
+                stage(k, i)
             if live(n):
                 scale_similarity(n)
-            if live(n - 3):
-                quantise_e(n - 3)
-                invert_weight(n - 3)
-            if live(n):
-                find_maximum(n)
+            t = n - 3
+            if live(t):
+                if t >= TILES - CHUNK:
+                    quantise_e(t, 1)
+                elif t % 2 == 2 - 1:
+                    quantise_e(t - 1, 2)
+                invert_weight(t)
+            if live(n - 4):
+                multiply_attracted(n - 4)
             if n == 1:
                 quantise_current(1)
             if n in (2, 3):
                 quantise_rows(n - 2)
-            if more and q == 2:
-                quantise_current(k + 1)
-            if live(n - 5) and not on_scalar(n - 5):
-                finish_on_vector(n - 5)
-            if live(n - 5):
-                store(n - 5)
             if live(n):
-                fifth(n)
+                find_maximum(n)
+            for stage, k, i in now:
+                if stage == regroup_current and i == 1:
+                    quantise_current(k)
+            if live(n - 6) and not on_scalar(n - 6):
+                finish_on_vector(n - 6)
+            if live(n - 6):
+                store(n - 6)
             if live(n - 1):
                 exponent(n - 1)
                 weigh(n - 1)
+            if live(n):
+                fifth(n)
             if live(n - 2):
                 regroup_e(n - 2)

@@ -18,7 +18,7 @@ TILES = B // P
 CHUNK = 4
 CHUNKS = TILES // CHUNK
 EPS = 1e-8
-PREP_SLOTS = 26
+PREP_SLOTS = 24
 FLOPS = 2 * B * C * D * 2
 
 
@@ -57,18 +57,33 @@ def tile_ca3_recurrentmatrix_pa_t_kernel(tc, current, memory_matrix, out):
         make_identity(nc, ident[:])
         one = keep.tile([P, 1], F32)
         nc.vector.memset(one[:], 1.0)
-        minus_half = keep.tile([P, 8], F32)
+        minus_half = keep.tile([P, 2 * CHUNK], F32)
         nc.vector.memset(minus_half[:], -0.5)
         warm = keep.tile([P, 1], F32)
-        nc.scalar.activation(out=warm[:], in_=one[:], func=FN.Exp)
+        nc.scalar.activation(out=warm[:], in_=one[:], func=FN.Sqrt)
 
         def sum_squares(dst, row):
             junk = junkp.tile([P, D], BF16)
             nc.scalar.activation(out=junk[:], in_=row, func=FN.Square, accum_out=dst)
 
-        def inverse_norms(ss, n, name):
+        def floored(ss, n, name):
             floor = keep.tile([P, n], F32, name="floor_" + name)
-            nc.gpsimd.tensor_scalar(out=floor[:], in0=ss, scalar1=EPS * EPS, scalar2=1.0, op0=ALU.max, op1=ALU.mult)
+            nc.gpsimd.tensor_scalar(out=floor[:], in0=ss[:], scalar1=EPS * EPS, scalar2=1.0, op0=ALU.max, op1=ALU.mult)
+            return floor
+
+        def norms_on_scalar(floor, n, name):
+            norm = keep.tile([P, n], F32, name="norm_" + name)
+            nc.scalar.activation(out=norm[:], in_=floor[:], func=FN.Sqrt)
+            return norm
+
+        def inverse_on_vector(norm, n, name):
+            inv = keep.tile([P, n], F32, name="inv_" + name)
+            nc.vector.reciprocal(out=inv[:], in_=norm[:])
+            return inv
+
+        def inverse_on_gpsimd(ss, n, name):
+            floor = keep.tile([P, n], F32, name="floor_" + name)
+            nc.gpsimd.tensor_scalar(out=floor[:], in0=ss[:], scalar1=EPS * EPS, scalar2=1.0, op0=ALU.max, op1=ALU.mult)
             inv = keep.tile([P, n], F32, name="inv_" + name)
             nc.gpsimd.tensor_tensor(out=inv[:], in0=floor[:], in1=minus_half[:, 0:n], op=ALU.pow)
             return inv
@@ -104,21 +119,25 @@ def tile_ca3_recurrentmatrix_pa_t_kernel(tc, current, memory_matrix, out):
             c_codes[k] = codes
             c_scales[k] = scales
 
+        groups = ((0,), (1,), (2, 3), (4, 5), (6, 7))
+        group_of = {}
+        for g, chunks in enumerate(groups):
+            for s, k in enumerate(chunks):
+                group_of[k] = (g, s)
+
         def square_current(k, i):
-            pair, s = divmod(i, 2)
-            if s == 0:
-                ss = keep.tile([P, 2], F32, name="c_ss%d_%d" % (k, pair))
-                c_ss[k, pair] = ss
-            sum_squares(c_ss[k, pair][:, s : s + 1], cur_sb[k][:, D * i : D * (i + 1)])
-            if s == 1:
-                c_inv[k, pair] = inverse_norms(c_ss[k, pair][:], 2, "c%d_%d" % (k, pair))
+            g, s = group_of[k]
+            if s == 0 and i == 0:
+                ss = keep.tile([P, CHUNK * len(groups[g])], F32, name="c_ss%d" % g)
+                c_ss[g] = ss
+            col = CHUNK * s + i
+            sum_squares(c_ss[g][:, col : col + 1], cur_sb[k][:, D * i : D * (i + 1)])
+            if g >= 2 and s == len(groups[g]) - 1 and i == CHUNK - 1:
+                c_inv[g] = inverse_on_gpsimd(c_ss[g], CHUNK * len(groups[g]), "c%d" % g)
 
         mem_w = mem_sb[:].bitcast(F32)
-        m_ss = []
+        m_ss = keep.tile([P, 8], F32)
         m_r = []
-        for h in range(2):
-            ss = keep.tile([P, 4], F32, name="m_ss%d" % h)
-            m_ss.append(ss)
         g_m = keep.tile([P, 4 * C], BF16, align_bytes=64)
         m_codes = keep.tile([P, C], U32, align_bytes=64)
         m_scales = keep.tile([P, C], U8, align_bytes=64)
@@ -129,23 +148,26 @@ def tile_ca3_recurrentmatrix_pa_t_kernel(tc, current, memory_matrix, out):
             g_kg = keep.tile([P, 4 * D], BF16, name="g_k%d" % g, align_bytes=64)
             g_k.append(g_kg)
         r_neg = keep.tile([P, C], F32)
+        m_banks = []
 
-        def square_memory(h):
-            for j in range(4):
-                row = mem_v[:, 4 * h + j, :]
-                if h == 0:
-                    sum_squares(m_ss[h][:, j : j + 1], row)
-                else:
-                    junk = junkp.tile([P, D], BF16, name="vjunk")
-                    nc.vector.scalar_tensor_tensor(
-                        out=junk[:], in0=row, scalar=1.0, in1=row, op0=ALU.mult, op1=ALU.mult, accum_out=m_ss[h][:, j : j + 1]
-                    )
-            m_r.append(inverse_norms(m_ss[h][:], 4, "m%d" % h))
+        def square_memory(j):
+            row = mem_v[:, j, :]
+            if j % 2 == 1:
+                sum_squares(m_ss[:, j : j + 1], row)
+            else:
+                junk = junkp.tile([P, D], BF16, name="vjunk")
+                nc.vector.scalar_tensor_tensor(
+                    out=junk[:], in0=row, scalar=1.0, in1=row, op0=ALU.mult, op1=ALU.mult, accum_out=m_ss[:, j : j + 1]
+                )
 
         def turn_memory(jp):
             bank = ps_sim.tile([P, 512], F32, tag="sim")
             for n in range(4):
                 nc.tensor.transpose(bank[:, n * P : (n + 1) * P], mem_w[:, 512 * jp + P * n : 512 * jp + P * (n + 1)], ident[:])
+            m_banks.append(bank)
+
+        def regroup_features(jp):
+            bank = m_banks[jp]
             dst = g_m[:].bitcast(F32)[:, 512 * jp : 512 * (jp + 1)].rearrange("q (b i u) -> q b i u", i=2, u=2)
             src = bank[:].rearrange("q (i u b) -> q b i u", i=2, u=2)
             if jp < 2:
@@ -161,13 +183,9 @@ def tile_ca3_recurrentmatrix_pa_t_kernel(tc, current, memory_matrix, out):
             )
 
         def regroup_memory(g):
-            nc.gpsimd.tensor_scalar(
+            nc.vector.tensor_copy(
                 out=g_k[g][:].rearrange("p (c i t) -> p c t i", i=4, t=4),
-                in0=mem_sb[:, 2048 * g : 2048 * (g + 1)].rearrange("p (t c i) -> p c t i", t=4, i=4),
-                scalar1=1.0,
-                scalar2=0.0,
-                op0=ALU.mult,
-                op1=ALU.add,
+                in_=mem_sb[:, 2048 * g : 2048 * (g + 1)].rearrange("p (t c i) -> p c t i", t=4, i=4),
             )
 
         def quantise_rows(g):
@@ -182,41 +200,16 @@ def tile_ca3_recurrentmatrix_pa_t_kernel(tc, current, memory_matrix, out):
         def spread_norms(h):
             bank = ps_sim.tile([P, 512], F32, tag="sim")
             for n in range(4):
-                nc.tensor.transpose(bank[:, n * P : (n + 1) * P], m_r[h][:, n : n + 1].to_broadcast([P, P]), ident[:])
+                nc.tensor.transpose(bank[:, n * P : (n + 1) * P], m_r[0][:, 4 * h + n : 4 * h + n + 1].to_broadcast([P, P]), ident[:])
             r_banks.append(bank)
 
         def keep_norms(h):
-            nc.vector.tensor_scalar_mul(
+            nc.scalar.activation(
                 out=r_neg[:, 512 * h : 512 * (h + 1)].rearrange("q (m b i) -> q m b i", m=2, i=2),
-                in0=r_banks[h][:].rearrange("q (m i b) -> q m b i", m=2, i=2),
-                scalar1=-1.0,
+                in_=r_banks[h][:].rearrange("q (m i b) -> q m b i", m=2, i=2),
+                func=FN.Copy,
+                scale=-1.0,
             )
-
-        square_memory(0)
-        turn_memory(0)
-        turn_memory(1)
-        square_memory(1)
-        turn_memory(2)
-        turn_memory(3)
-        for pr in range(2):
-            turn_current(0, pr)
-            regroup_current(0, pr)
-        for i in range(CHUNK):
-            square_current(0, i)
-        quantise_memory(0)
-        quantise_current(0)
-        quantise_memory(1)
-        spread_norms(0)
-        for pr in range(2):
-            turn_current(1, pr)
-            regroup_current(1, pr)
-        spread_norms(1)
-        keep_norms(0)
-        keep_norms(1)
-        for g in range(2):
-            regroup_memory(g)
-        for i in range(CHUNK):
-            square_current(1, i)
 
         sim_banks = {}
         ys = {}
@@ -255,7 +248,7 @@ def tile_ca3_recurrentmatrix_pa_t_kernel(tc, current, memory_matrix, out):
                 nc.vector.scalar_tensor_tensor(
                     out=y[:, 512 * h : 512 * (h + 1)],
                     in0=sim_banks[t, h][:],
-                    scalar=c_inv[k, i // 2][:, i % 2 : i % 2 + 1],
+                    scalar=c_inv[group_of[k][0]][:, CHUNK * group_of[k][1] + i : CHUNK * group_of[k][1] + i + 1],
                     in1=r_neg[:, 512 * h : 512 * (h + 1)],
                     op0=ALU.mult,
                     op1=ALU.mult,
@@ -338,7 +331,7 @@ def tile_ca3_recurrentmatrix_pa_t_kernel(tc, current, memory_matrix, out):
             accs[t] = acc
 
         def on_scalar(t):
-            return t < 27 and t % 6 != 2
+            return t < 27 and t % 3 != 2
 
         def output_half(t):
             if t % 2 == 0:
@@ -356,18 +349,55 @@ def tile_ca3_recurrentmatrix_pa_t_kernel(tc, current, memory_matrix, out):
             nc.vector.scalar_tensor_tensor(out=half, in0=accs[t][:], scalar=scs[t // 2][:, t % 2 : t % 2 + 1], in1=fifths[t][:], op0=ALU.mult, op1=ALU.add)
 
         def store(t):
-            if t % 2 == 1:
+            if t >= TILES - 2:
+                nc.sync.dma_start(out=out_rows[:, D * t : D * (t + 1)], in_=outs[t // 2][:, D * (t % 2) : D * (t % 2 + 1)])
+            elif t % 2 == 1:
                 nc.sync.dma_start(out=out_rows[:, D * (t - 1) : D * (t + 1)], in_=outs[t // 2][:])
 
         def live(t):
             return 0 <= t < TILES
 
-        pieces = []
-        for k in range(2, CHUNKS):
-            pieces += [(regroup_current, k, 0), (regroup_current, k, 1)] + [(square_current, k, i) for i in range(CHUNK)]
-        done = 0
+        for j in range(8):
+            square_memory(j)
+        for jp in range(4):
+            turn_memory(jp)
+        m_floor = floored(m_ss, 8, "m")
+        for jp in (2, 3, 0, 1):
+            regroup_features(jp)
+        for pr in range(2):
+            turn_current(0, pr)
+        m_norm = norms_on_scalar(m_floor, 8, "m")
+        for pr in range(2):
+            regroup_current(0, pr)
+        m_r.append(inverse_on_vector(m_norm, 8, "m"))
+        quantise_memory(0)
+        spread_norms(0)
+        spread_norms(1)
+        for i in range(CHUNK):
+            square_current(0, i)
+        keep_norms(0)
+        keep_norms(1)
+        quantise_current(0)
+        quantise_memory(1)
+        for g in range(2):
+            regroup_memory(g)
+        c_floor = floored(c_ss[0], CHUNK, "c0")
+        c_norm = norms_on_scalar(c_floor, CHUNK, "c0")
+        c_inv[0] = inverse_on_vector(c_norm, CHUNK, "c0")
         multiply_similarity(0)
-        for n in range(TILES + 7):
+        for pr in range(2):
+            turn_current(1, pr)
+        for i in range(CHUNK):
+            square_current(1, i)
+        for pr in range(2):
+            regroup_current(1, pr)
+
+        pieces = []
+        for k in range(2, CHUNKS, 2):
+            pieces += [(square_current, k + j, i) for j in range(2) for i in range(CHUNK)]
+            pieces += [(regroup_current, k + j, pr) for j in range(2) for pr in range(2)]
+        done = 0
+        for n in range(TILES + 6):
             now = pieces[done : (n + 1) * len(pieces) // PREP_SLOTS]
             done += len(now)
             later = pieces[done : (n + 2) * len(pieces) // PREP_SLOTS]
@@ -378,8 +408,8 @@ def tile_ca3_recurrentmatrix_pa_t_kernel(tc, current, memory_matrix, out):
             for stage, k, i in (now + later if n == 0 else later):
                 if stage == regroup_current:
                     turn_current(k, i)
-            if live(n - 6) and on_scalar(n - 6):
-                finish_on_scalar(n - 6)
+            if live(n - 5) and on_scalar(n - 5):
+                finish_on_scalar(n - 5)
             for stage, k, i in now:
                 stage(k, i)
             if live(n):
@@ -391,21 +421,27 @@ def tile_ca3_recurrentmatrix_pa_t_kernel(tc, current, memory_matrix, out):
                 elif t % 2 == 2 - 1:
                     quantise_e(t - 1, 2)
                 invert_weight(t)
-            if live(n - 4):
-                multiply_attracted(n - 4)
-            if n == 1:
-                quantise_current(1)
             if n in (2, 3):
                 quantise_rows(n - 2)
+            if live(n - 4):
+                multiply_attracted(n - 4)
+            if n == 0:
+                c_floor = floored(c_ss[1], CHUNK, "c1")
+            if n == 1:
+                c_norm = norms_on_scalar(c_floor, CHUNK, "c1")
             if live(n):
                 find_maximum(n)
+            if n == 1:
+                quantise_current(1)
+            if n == 2:
+                c_inv[1] = inverse_on_vector(c_norm, CHUNK, "c1")
             for stage, k, i in now:
                 if stage == regroup_current and i == 1:
                     quantise_current(k)
-            if live(n - 6) and not on_scalar(n - 6):
-                finish_on_vector(n - 6)
-            if live(n - 6):
-                store(n - 6)
+            if live(n - 5) and not on_scalar(n - 5):
+                finish_on_vector(n - 5)
+            if live(n - 5):
+                store(n - 5)
             if live(n - 1):
                 exponent(n - 1)
                 weigh(n - 1)

@@ -18,7 +18,7 @@ TILES = B // P
 CHUNK = 4
 CHUNKS = TILES // CHUNK
 EPS = 1e-8
-PREP_SLOTS = 24
+PREP_SLOTS = 23
 FLOPS = 2 * B * C * D * 2
 
 
@@ -33,7 +33,7 @@ def tile_ca3_recurrentmatrix_pa_t_kernel(tc, current, memory_matrix, out):
         junkp = stack.enter_context(tc.tile_pool(name="junkp", bufs=2))
         gcp = stack.enter_context(tc.tile_pool(name="gcp", bufs=2))
         c02p = stack.enter_context(tc.tile_pool(name="c02p", bufs=11))
-        yp = stack.enter_context(tc.tile_pool(name="yp", bufs=4))
+        yp = stack.enter_context(tc.tile_pool(name="yp", bufs=5))
         ep = stack.enter_context(tc.tile_pool(name="ep", bufs=3))
         small = stack.enter_context(tc.tile_pool(name="small", bufs=10))
         gep = stack.enter_context(tc.tile_pool(name="gep", bufs=2))
@@ -240,19 +240,17 @@ def tile_ca3_recurrentmatrix_pa_t_kernel(tc, current, memory_matrix, out):
                 )
                 sim_banks[t, h] = ps
 
-        def scale_similarity(t):
+        def scale_similarity(t, h):
             k, i = divmod(t, CHUNK)
-            y = yp.tile([P, C], F32)
-            ys[t] = y
-            for h in range(2):
-                nc.vector.scalar_tensor_tensor(
-                    out=y[:, 512 * h : 512 * (h + 1)],
-                    in0=sim_banks[t, h][:],
-                    scalar=c_inv[group_of[k][0]][:, CHUNK * group_of[k][1] + i : CHUNK * group_of[k][1] + i + 1],
-                    in1=r_neg[:, 512 * h : 512 * (h + 1)],
-                    op0=ALU.mult,
-                    op1=ALU.mult,
-                )
+            g, s = group_of[k]
+            if h == 0:
+                y = yp.tile([P, C], F32)
+                ys[t] = y
+            half = slice(512 * h, 512 * (h + 1))
+            col = CHUNK * s + i
+            nc.vector.scalar_tensor_tensor(
+                out=ys[t][:, half], in0=sim_banks[t, h][:], scalar=c_inv[g][:, col : col + 1], in1=r_neg[:, half], op0=ALU.mult, op1=ALU.mult
+            )
 
         def find_maximum(t):
             nb = small.tile([P, 1], F32)
@@ -331,7 +329,7 @@ def tile_ca3_recurrentmatrix_pa_t_kernel(tc, current, memory_matrix, out):
             accs[t] = acc
 
         def on_scalar(t):
-            return t < 27 and t % 3 != 2
+            return t < 27 and t % 4 != 2
 
         def output_half(t):
             if t % 2 == 0:
@@ -397,24 +395,33 @@ def tile_ca3_recurrentmatrix_pa_t_kernel(tc, current, memory_matrix, out):
             pieces += [(square_current, k + j, i) for j in range(2) for i in range(CHUNK)]
             pieces += [(regroup_current, k + j, pr) for j in range(2) for pr in range(2)]
         done = 0
-        for n in range(TILES + 6):
+        for n in range(TILES + 8):
             now = pieces[done : (n + 1) * len(pieces) // PREP_SLOTS]
             done += len(now)
             later = pieces[done : (n + 2) * len(pieces) // PREP_SLOTS]
-            if live(n - 2):
-                transpose_e(n - 2)
+            if live(n - 3):
+                transpose_e(n - 3)
             if live(n + 1):
                 multiply_similarity(n + 1)
             for stage, k, i in (now + later if n == 0 else later):
                 if stage == regroup_current:
                     turn_current(k, i)
-            if live(n - 5) and on_scalar(n - 5):
-                finish_on_scalar(n - 5)
+            if live(n - 7) and on_scalar(n - 7):
+                finish_on_scalar(n - 7)
             for stage, k, i in now:
                 stage(k, i)
+            if live(n - 2):
+                exponent(n - 2)
+                weigh(n - 2)
+            if live(n - 3):
+                regroup_e(n - 3)
             if live(n):
-                scale_similarity(n)
-            t = n - 3
+                scale_similarity(n, 0)
+            if live(n - 1):
+                find_maximum(n - 1)
+            if live(n):
+                scale_similarity(n, 1)
+            t = n - 4
             if live(t):
                 if t >= TILES - CHUNK:
                     quantise_e(t, 1)
@@ -423,14 +430,12 @@ def tile_ca3_recurrentmatrix_pa_t_kernel(tc, current, memory_matrix, out):
                 invert_weight(t)
             if n in (2, 3):
                 quantise_rows(n - 2)
-            if live(n - 4):
-                multiply_attracted(n - 4)
+            if live(n - 5):
+                multiply_attracted(n - 5)
             if n == 0:
                 c_floor = floored(c_ss[1], CHUNK, "c1")
             if n == 1:
                 c_norm = norms_on_scalar(c_floor, CHUNK, "c1")
-            if live(n):
-                find_maximum(n)
             if n == 1:
                 quantise_current(1)
             if n == 2:
@@ -438,14 +443,9 @@ def tile_ca3_recurrentmatrix_pa_t_kernel(tc, current, memory_matrix, out):
             for stage, k, i in now:
                 if stage == regroup_current and i == 1:
                     quantise_current(k)
-            if live(n - 5) and not on_scalar(n - 5):
-                finish_on_vector(n - 5)
-            if live(n - 5):
-                store(n - 5)
-            if live(n - 1):
-                exponent(n - 1)
-                weigh(n - 1)
+            if live(n - 7) and not on_scalar(n - 7):
+                finish_on_vector(n - 7)
+            if live(n - 7):
+                store(n - 7)
             if live(n):
                 fifth(n)
-            if live(n - 2):
-                regroup_e(n - 2)

@@ -18,7 +18,7 @@ TILES = B // P
 CHUNK = 4
 CHUNKS = TILES // CHUNK
 EPS = 1e-8
-PREP_SLOTS = 23
+PREP_SLOTS = 24
 FLOPS = 2 * B * C * D * 2
 
 
@@ -395,7 +395,7 @@ def tile_ca3_recurrentmatrix_pa_t_kernel(tc, current, memory_matrix, out):
             pieces += [(square_current, k + j, i) for j in range(2) for i in range(CHUNK)]
             pieces += [(regroup_current, k + j, pr) for j in range(2) for pr in range(2)]
         done = 0
-        for n in range(TILES + 8):
+        for n in range(TILES + 7):
             now = pieces[done : (n + 1) * len(pieces) // PREP_SLOTS]
             done += len(now)
             later = pieces[done : (n + 2) * len(pieces) // PREP_SLOTS]
@@ -406,8 +406,6 @@ def tile_ca3_recurrentmatrix_pa_t_kernel(tc, current, memory_matrix, out):
             for stage, k, i in (now + later if n == 0 else later):
                 if stage == regroup_current:
                     turn_current(k, i)
-            if live(n - 7) and on_scalar(n - 7):
-                finish_on_scalar(n - 7)
             for stage, k, i in now:
                 stage(k, i)
             if live(n - 2):
@@ -415,12 +413,16 @@ def tile_ca3_recurrentmatrix_pa_t_kernel(tc, current, memory_matrix, out):
                 weigh(n - 2)
             if live(n - 3):
                 regroup_e(n - 3)
+            if live(n - 6) and on_scalar(n - 6):
+                finish_on_scalar(n - 6)
             if live(n):
                 scale_similarity(n, 0)
             if live(n - 1):
                 find_maximum(n - 1)
             if live(n):
                 scale_similarity(n, 1)
+            if live(n - 6) and not on_scalar(n - 6):
+                finish_on_vector(n - 6)
             t = n - 4
             if live(t):
                 if t >= TILES - CHUNK:
@@ -443,9 +445,7 @@ def tile_ca3_recurrentmatrix_pa_t_kernel(tc, current, memory_matrix, out):
             for stage, k, i in now:
                 if stage == regroup_current and i == 1:
                     quantise_current(k)
-            if live(n - 7) and not on_scalar(n - 7):
-                finish_on_vector(n - 7)
-            if live(n - 7):
-                store(n - 7)
+            if live(n - 6):
+                store(n - 6)
             if live(n):
                 fifth(n)

from contextlib import ExitStack

import concourse.mybir as mybir
from concourse.masks import make_identity

F32 = mybir.dt.float32
BF16 = mybir.dt.bfloat16
U32 = mybir.dt.uint32
U8 = mybir.dt.uint8
FP8X4 = mybir.dt.float8_e4m3fn_x4
ALU = mybir.AluOpType
FN = mybir.ActivationFunctionType
AXIS_X = mybir.AxisListType.X

P = 128
B, C, D = 4096, 1024, 512
TILES = B // P
CHUNK = 4
CHUNKS = TILES // CHUNK
EPS = 1e-8
PREP_SLOTS = 24
FLOPS = 2 * B * C * D * 2


def tile_ca3_recurrentmatrix_pa_t_kernel(tc, current, memory_matrix, out):
    nc = tc.nc
    cur_rows = current.rearrange("(p t) d -> p (t d)", t=TILES)
    out_rows = out.rearrange("(p t) d -> p (t d)", t=TILES)
    mem_rows = memory_matrix.rearrange("(j p) d -> p j d", p=P)

    with ExitStack() as stack:
        keep = stack.enter_context(tc.tile_pool(name="keep", bufs=1))
        junkp = stack.enter_context(tc.tile_pool(name="junkp", bufs=2))
        gcp = stack.enter_context(tc.tile_pool(name="gcp", bufs=2))
        c02p = stack.enter_context(tc.tile_pool(name="c02p", bufs=11))
        yp = stack.enter_context(tc.tile_pool(name="yp", bufs=5))
        ep = stack.enter_context(tc.tile_pool(name="ep", bufs=3))
        small = stack.enter_context(tc.tile_pool(name="small", bufs=10))
        gep = stack.enter_context(tc.tile_pool(name="gep", bufs=2))
        op = stack.enter_context(tc.tile_pool(name="op", bufs=4))
        ps_sim = stack.enter_context(tc.psum_pool(name="ps_sim", bufs=4))
        ps_tr = stack.enter_context(tc.psum_pool(name="ps_tr", bufs=2))
        ps_acc = stack.enter_context(tc.psum_pool(name="ps_acc", bufs=2))
        stack.enter_context(tc.manual_schedule())

        mem_sb = keep.tile([P, 8 * D], BF16)
        mem_v = mem_sb[:].rearrange("p (j d) -> p j d", j=8)
        for h in range(4):
            nc.sync.dma_start(out=mem_v[:, 2 * h : 2 * h + 2, :], in_=mem_rows[:, 2 * h : 2 * h + 2, :])
        cur_sb = []
        for k in range(CHUNKS):
            cur_k = keep.tile([P, CHUNK * D], BF16, name="cur%d" % k)
            nc.sync.dma_start(out=cur_k[:], in_=cur_rows[:, k * CHUNK * D : (k + 1) * CHUNK * D])
            cur_sb.append(cur_k)

        ident = keep.tile([P, P], F32)
        make_identity(nc, ident[:])
        one = keep.tile([P, 1], F32)
        nc.vector.memset(one[:], 1.0)
        minus_half = keep.tile([P, 2 * CHUNK], F32)
        nc.vector.memset(minus_half[:], -0.5)
        warm = keep.tile([P, 1], F32)
        nc.scalar.activation(out=warm[:], in_=one[:], func=FN.Sqrt)

        def sum_squares(dst, row):
            junk = junkp.tile([P, D], BF16)
            nc.scalar.activation(out=junk[:], in_=row, func=FN.Square, accum_out=dst)

        def floored(ss, n, name):
            floor = keep.tile([P, n], F32, name="floor_" + name)
            nc.gpsimd.tensor_scalar(out=floor[:], in0=ss[:], scalar1=EPS * EPS, scalar2=1.0, op0=ALU.max, op1=ALU.mult)
            return floor

        def norms_on_scalar(floor, n, name):
            norm = keep.tile([P, n], F32, name="norm_" + name)
            nc.scalar.activation(out=norm[:], in_=floor[:], func=FN.Sqrt)
            return norm

        def inverse_on_vector(norm, n, name):
            inv = keep.tile([P, n], F32, name="inv_" + name)
            nc.vector.reciprocal(out=inv[:], in_=norm[:])
            return inv

        def inverse_on_gpsimd(ss, n, name):
            floor = keep.tile([P, n], F32, name="floor_" + name)
            nc.gpsimd.tensor_scalar(out=floor[:], in0=ss[:], scalar1=EPS * EPS, scalar2=1.0, op0=ALU.max, op1=ALU.mult)
            inv = keep.tile([P, n], F32, name="inv_" + name)
            nc.gpsimd.tensor_tensor(out=inv[:], in0=floor[:], in1=minus_half[:, 0:n], op=ALU.pow)
            return inv

        g_cs = {}
        c_banks = {}
        c_codes = {}
        c_scales = {}
        c_ss = {}
        c_inv = {}

        def turn_current(k, pr):
            if pr == 0:
                g_c = gcp.tile([P, CHUNK * D], BF16, align_bytes=64)
                g_cs[k] = g_c
            cw = cur_sb[k][:].bitcast(F32)
            bank = ps_tr.tile([P, 512], F32, tag="tr")
            for n in range(4):
                nc.tensor.transpose(bank[:, n * P : (n + 1) * P], cw[:, 512 * pr + P * n : 512 * pr + P * (n + 1)], ident[:])
            c_banks[k, pr] = bank

        def regroup_current(k, pr):
            bank = c_banks[k, pr]
            nc.scalar.copy(
                out=g_cs[k][:].bitcast(F32)[:, 512 * pr : 512 * (pr + 1)].rearrange("q (i b u) -> q i b u", i=2, u=2),
                in_=bank[:].rearrange("q (i u b) -> q i b u", i=2, u=2),
            )

        def quantise_current(k):
            codes = keep.tile([P, CHUNK * P], U32, name="c_codes%d" % k, align_bytes=64)
            scales = keep.tile([P, CHUNK * P], U8, name="c_scales%d" % k, align_bytes=64)
            nc.vector.quantize_mx(out=codes[:].bitcast(FP8X4), scales=scales[:], in_=g_cs[k][:])
            c_codes[k] = codes
            c_scales[k] = scales

        groups = ((0,), (1,), (2, 3), (4, 5), (6, 7))
        group_of = {}
        for g, chunks in enumerate(groups):
            for s, k in enumerate(chunks):
                group_of[k] = (g, s)

        def square_current(k, i):
            g, s = group_of[k]
            if s == 0 and i == 0:
                ss = keep.tile([P, CHUNK * len(groups[g])], F32, name="c_ss%d" % g)
                c_ss[g] = ss
            col = CHUNK * s + i
            sum_squares(c_ss[g][:, col : col + 1], cur_sb[k][:, D * i : D * (i + 1)])
            if g >= 2 and s == len(groups[g]) - 1 and i == CHUNK - 1:
                c_inv[g] = inverse_on_gpsimd(c_ss[g], CHUNK * len(groups[g]), "c%d" % g)

        mem_w = mem_sb[:].bitcast(F32)
        m_ss = keep.tile([P, 8], F32)
        m_r = []
        g_m = keep.tile([P, 4 * C], BF16, align_bytes=64)
        m_codes = keep.tile([P, C], U32, align_bytes=64)
        m_scales = keep.tile([P, C], U8, align_bytes=64)
        k_codes = keep.tile([P, 2 * D], U32, align_bytes=64)
        k_scales = keep.tile([P, 2 * D], U8, align_bytes=64)
        g_k = []
        for g in range(2):
            g_kg = keep.tile([P, 4 * D], BF16, name="g_k%d" % g, align_bytes=64)
            g_k.append(g_kg)
        r_neg = keep.tile([P, C], F32)
        m_banks = []

        def square_memory(j):
            row = mem_v[:, j, :]
            if j % 2 == 1:
                sum_squares(m_ss[:, j : j + 1], row)
            else:
                junk = junkp.tile([P, D], BF16, name="vjunk")
                nc.vector.scalar_tensor_tensor(
                    out=junk[:], in0=row, scalar=1.0, in1=row, op0=ALU.mult, op1=ALU.mult, accum_out=m_ss[:, j : j + 1]
                )

        def turn_memory(jp):
            bank = ps_sim.tile([P, 512], F32, tag="sim")
            for n in range(4):
                nc.tensor.transpose(bank[:, n * P : (n + 1) * P], mem_w[:, 512 * jp + P * n : 512 * jp + P * (n + 1)], ident[:])
            m_banks.append(bank)

        def regroup_features(jp):
            bank = m_banks[jp]
            dst = g_m[:].bitcast(F32)[:, 512 * jp : 512 * (jp + 1)].rearrange("q (b i u) -> q b i u", i=2, u=2)
            src = bank[:].rearrange("q (i u b) -> q b i u", i=2, u=2)
            if jp < 2:
                nc.vector.tensor_copy(out=dst, in_=src)
            else:
                nc.scalar.copy(out=dst, in_=src)

        def quantise_memory(h):
            nc.vector.quantize_mx(
                out=m_codes[:, 512 * h : 512 * (h + 1)].bitcast(FP8X4),
                scales=m_scales[:, 512 * h : 512 * (h + 1)],
                in_=g_m[:, 2048 * h : 2048 * (h + 1)],
            )

        def regroup_memory(g):
            nc.vector.tensor_copy(
                out=g_k[g][:].rearrange("p (c i t) -> p c t i", i=4, t=4),
                in_=mem_sb[:, 2048 * g : 2048 * (g + 1)].rearrange("p (t c i) -> p c t i", t=4, i=4),
            )

        def quantise_rows(g):
            nc.vector.quantize_mx(
                out=k_codes[:, D * g : D * (g + 1)].bitcast(FP8X4),
                scales=k_scales[:, D * g : D * (g + 1)],
                in_=g_k[g][:],
            )

        r_banks = []

        def spread_norms(h):
            bank = ps_sim.tile([P, 512], F32, tag="sim")
            for n in range(4):
                nc.tensor.transpose(bank[:, n * P : (n + 1) * P], m_r[0][:, 4 * h + n : 4 * h + n + 1].to_broadcast([P, P]), ident[:])
            r_banks.append(bank)

        def keep_norms(h):
            nc.scalar.activation(
                out=r_neg[:, 512 * h : 512 * (h + 1)].rearrange("q (m b i) -> q m b i", m=2, i=2),
                in_=r_banks[h][:].rearrange("q (m i b) -> q m b i", m=2, i=2),
                func=FN.Copy,
                scale=-1.0,
            )

        sim_banks = {}
        ys = {}
        nbs = {}
        es = {}
        rss = {}
        e_banks = {}
        ges = {}
        ecs = {}
        accs = {}
        scs = {}
        bigs = {}
        fifths = {}
        outs = {}

        def multiply_similarity(t):
            k, i = divmod(t, CHUNK)
            for h in range(2):
                ps = ps_sim.tile([P, 512], F32, tag="sim")
                nc.tensor.matmul_mx(
                    out=ps[:],
                    lhsT=c_codes[k][:, P * i : P * (i + 1)].bitcast(FP8X4),
                    lhsT_scale=c_scales[k][:, P * i : P * (i + 1)],
                    rhs=m_codes[:, 512 * h : 512 * (h + 1)].bitcast(FP8X4),
                    rhs_scale=m_scales[:, 512 * h : 512 * (h + 1)],
                    start=True,
                    stop=True,
                )
                sim_banks[t, h] = ps

        def scale_similarity(t, h):
            k, i = divmod(t, CHUNK)
            g, s = group_of[k]
            if h == 0:
                y = yp.tile([P, C], F32)
                ys[t] = y
            half = slice(512 * h, 512 * (h + 1))
            col = CHUNK * s + i
            nc.vector.scalar_tensor_tensor(
                out=ys[t][:, half], in0=sim_banks[t, h][:], scalar=c_inv[g][:, col : col + 1], in1=r_neg[:, half], op0=ALU.mult, op1=ALU.mult
            )

        def find_maximum(t):
            nb = small.tile([P, 1], F32)
            nc.vector.tensor_reduce(out=nb[:], in_=ys[t][:], axis=AXIS_X, op=ALU.min)
            nbs[t] = nb

        def exponent(t):
            e = ep.tile([P, C], BF16)
            if t % 2 == 0:
                rs = small.tile([P, 2], F32)
                rss[t // 2] = rs
            nc.scalar.activation(
                out=e[:], in_=ys[t][:], func=FN.Exp, bias=nbs[t][:], scale=-1.0, accum_out=rss[t // 2][:, t % 2 : t % 2 + 1]
            )
            es[t] = e

        def transpose_e(t):
            bank = ps_tr.tile([P, 512], F32, tag="tr")
            e_w = es[t][:].bitcast(F32)
            for n in range(4):
                nc.tensor.transpose(bank[:, n * P : (n + 1) * P], e_w[:, n * P : (n + 1) * P], ident[:])
            e_banks[t] = bank

        def regroup_e(t):
            k, i = divmod(t, CHUNK)
            if i == 0:
                g_e = gep.tile([P, CHUNK * C], BF16, align_bytes=64)
                ges[k] = g_e
            nc.scalar.copy(
                out=ges[k][:].bitcast(F32)[:, 512 * i : 512 * (i + 1)].rearrange("p (g b u) -> p g b u", g=2, u=2),
                in_=e_banks[t][:].rearrange("p (g u b) -> p g b u", g=2, u=2),
            )

        def quantise_e(t, tiles):
            k, i = divmod(t, CHUNK)
            if k not in ecs:
                e_codes = gep.tile([P, CHUNK * 2 * P], U32, align_bytes=64)
                e_scales = gep.tile([P, CHUNK * 2 * P], U8, align_bytes=64)
                ecs[k] = (e_codes, e_scales)
            e_codes, e_scales = ecs[k]
            words = slice(2 * P * i, 2 * P * (i + tiles))
            nc.vector.quantize_mx(out=e_codes[:, words].bitcast(FP8X4), scales=e_scales[:, words], in_=ges[k][:, C * i : C * (i + tiles)])

        def weigh(t):
            if t % 2 == 1:
                big = small.tile([P, 2], F32)
                nc.gpsimd.tensor_scalar(out=big[:], in0=rss[t // 2][:], scalar1=1.25, scalar2=0.0, op0=ALU.mult, op1=ALU.add)
                bigs[t // 2] = big

        def invert_weight(t):
            if t % 2 == 1:
                sc = small.tile([P, 2], F32)
                nc.vector.reciprocal(out=sc[:], in_=bigs[t // 2][:])
                scs[t // 2] = sc

        def fifth(t):
            k, i = divmod(t, CHUNK)
            c02 = c02p.tile([P, D], F32)
            nc.gpsimd.tensor_scalar(out=c02[:], in0=cur_sb[k][:, D * i : D * (i + 1)], scalar1=0.2, scalar2=0.0, op0=ALU.mult, op1=ALU.add)
            fifths[t] = c02

        def multiply_attracted(t):
            e_codes, e_scales = ecs[t // CHUNK]
            acc = ps_acc.tile([P, D], F32)
            for g in range(2):
                w = 2 * (t % CHUNK) + g
                nc.tensor.matmul_mx(
                    out=acc[:],
                    lhsT=e_codes[:, P * w : P * (w + 1)].bitcast(FP8X4),
                    lhsT_scale=e_scales[:, P * w : P * (w + 1)],
                    rhs=k_codes[:, D * g : D * (g + 1)].bitcast(FP8X4),
                    rhs_scale=k_scales[:, D * g : D * (g + 1)],
                    start=(g == 0),
                    stop=(g == 1),
                )
            accs[t] = acc

        def on_scalar(t):
            return t < 27 and t % 4 != 2

        def output_half(t):
            if t % 2 == 0:
                o = op.tile([P, 2 * D], F32)
                outs[t // 2] = o
            return outs[t // 2][:, D * (t % 2) : D * (t % 2 + 1)]

        def finish_on_scalar(t):
            half = output_half(t)
            nc.scalar.activation(out=half, in_=accs[t][:], func=FN.Copy, scale=scs[t // 2][:, t % 2 : t % 2 + 1])
            nc.gpsimd.tensor_tensor(out=half, in0=half, in1=fifths[t][:], op=ALU.add)

        def finish_on_vector(t):
            half = output_half(t)
            nc.vector.scalar_tensor_tensor(out=half, in0=accs[t][:], scalar=scs[t // 2][:, t % 2 : t % 2 + 1], in1=fifths[t][:], op0=ALU.mult, op1=ALU.add)

        def store(t):
            if t >= TILES - 2:
                nc.sync.dma_start(out=out_rows[:, D * t : D * (t + 1)], in_=outs[t // 2][:, D * (t % 2) : D * (t % 2 + 1)])
            elif t % 2 == 1:
                nc.sync.dma_start(out=out_rows[:, D * (t - 1) : D * (t + 1)], in_=outs[t // 2][:])

        def live(t):
            return 0 <= t < TILES

        for j in range(8):
            square_memory(j)
        for jp in range(4):
            turn_memory(jp)
        m_floor = floored(m_ss, 8, "m")
        for jp in (2, 3, 0, 1):
            regroup_features(jp)
        for pr in range(2):
            turn_current(0, pr)
        m_norm = norms_on_scalar(m_floor, 8, "m")
        for pr in range(2):
            regroup_current(0, pr)
        m_r.append(inverse_on_vector(m_norm, 8, "m"))
        quantise_memory(0)
        spread_norms(0)
        spread_norms(1)
        for i in range(CHUNK):
            square_current(0, i)
        keep_norms(0)
        keep_norms(1)
        quantise_current(0)
        quantise_memory(1)
        for g in range(2):
            regroup_memory(g)
        c_floor = floored(c_ss[0], CHUNK, "c0")
        c_norm = norms_on_scalar(c_floor, CHUNK, "c0")
        c_inv[0] = inverse_on_vector(c_norm, CHUNK, "c0")
        multiply_similarity(0)
        for pr in range(2):
            turn_current(1, pr)
        for i in range(CHUNK):
            square_current(1, i)
        for pr in range(2):
            regroup_current(1, pr)

        pieces = []
        for k in range(2, CHUNKS, 2):
            pieces += [(square_current, k + j, i) for j in range(2) for i in range(CHUNK)]
            pieces += [(regroup_current, k + j, pr) for j in range(2) for pr in range(2)]
        done = 0
        for n in range(TILES + 7):
            now = pieces[done : (n + 1) * len(pieces) // PREP_SLOTS]
            done += len(now)
            later = pieces[done : (n + 2) * len(pieces) // PREP_SLOTS]
            if live(n - 3):
                transpose_e(n - 3)
            if live(n + 1):
                multiply_similarity(n + 1)
            for stage, k, i in (now + later if n == 0 else later):
                if stage == regroup_current:
                    turn_current(k, i)
            for stage, k, i in now:
                stage(k, i)
            if live(n - 2):
                exponent(n - 2)
                weigh(n - 2)
            if live(n - 3):
                regroup_e(n - 3)
            if live(n - 6) and on_scalar(n - 6):
                finish_on_scalar(n - 6)
            if live(n):
                scale_similarity(n, 0)
            if live(n - 1):
                find_maximum(n - 1)
            if live(n):
                scale_similarity(n, 1)
            if live(n - 6) and not on_scalar(n - 6):
                finish_on_vector(n - 6)
            t = n - 4
            if live(t):
                if t >= TILES - CHUNK:
                    quantise_e(t, 1)
                elif t % 2 == 2 - 1:
                    quantise_e(t - 1, 2)
                invert_weight(t)
            if n in (2, 3):
                quantise_rows(n - 2)
            if live(n - 5):
                multiply_attracted(n - 5)
            if n == 0:
                c_floor = floored(c_ss[1], CHUNK, "c1")
            if n == 1:
                c_norm = norms_on_scalar(c_floor, CHUNK, "c1")
            if n == 1:
                quantise_current(1)
            if n == 2:
                c_inv[1] = inverse_on_vector(c_norm, CHUNK, "c1")
            for stage, k, i in now:
                if stage == regroup_current and i == 1:
                    quantise_current(k)
            if live(n - 6):
                store(n - 6)
            if live(n):
                fifth(n)
